import numpy as np
import ml_dtypes


def mxq(x, axis, fmt="e4m3"):
    dtype, down = {"e4m3": (ml_dtypes.float8_e4m3fn, 7), "e5m2": (ml_dtypes.float8_e5m2, 14)}[fmt]
    v = np.moveaxis(np.asarray(x, np.float32).astype(ml_dtypes.bfloat16).astype(np.float64), axis, -1)
    blocks = v.reshape(v.shape[:-1] + (-1, 32))
    amax = np.abs(blocks).max(-1, keepdims=True)
    byte = np.maximum(np.where(amax > 0, np.frexp(amax)[1] - 1 + 127, 0) - down, 1)
    scale = np.exp2(byte - 127.0)
    codes = (blocks / scale).astype(np.float32).astype(dtype).astype(np.float64)
    return np.moveaxis((codes * scale).reshape(v.shape), -1, axis)


WIDE = False


def mx_kscale(k):
    if not WIDE:
        return np.ones(k)
    levels = np.array([10, -10, 5, -5, 0])
    a = np.random.permutation(np.resize(levels, k // 512 * 4)).reshape(k // 512, 4)
    idx = np.arange(k)
    return np.exp2(a[idx // 512, idx % 128 // 32])


BF16 = ml_dtypes.bfloat16


def bf(x):
    return np.asarray(x, np.float32).astype(BF16)


def f64(x):
    return np.asarray(x).astype(np.float64)


E2M1 = np.array([0.0, 0.5, 1.0, 1.5, 2.0, 3.0, 4.0, 6.0, -0.0, -0.5, -1.0, -1.5, -2.0, -3.0, -4.0, -6.0])


def pack_weight(w, fmt):
    k, n = w.shape
    w = f64(bf(w)).reshape(k // 32, 32, n)
    amax = np.abs(w).max(1)
    if fmt == "e4m3":
        byte = np.frexp(amax)[1] - 1 + 127 - 7
    else:
        mant, ex = np.frexp(amax / 6.0)
        byte = np.where(mant > 0.5, ex, ex - 1) + 127
    byte = np.clip(np.where(amax > 0, byte, 1), 1, 254)
    scaled = (w * np.exp2(127.0 - byte)[:, None, :]).reshape(k, n).astype(np.float32)
    by_word = np.ascontiguousarray(scaled.reshape(k // 512, 128, 4, n).transpose(0, 1, 3, 2))
    if fmt == "e4m3":
        words = by_word.astype(ml_dtypes.float8_e4m3fn).view(np.uint8)
    else:
        c = by_word.astype(ml_dtypes.float4_e2m1fn).view(np.uint8) & 0xF
        words = c[..., 0::2] | (c[..., 1::2] << 4)
    return np.ascontiguousarray(words), np.ascontiguousarray(byte.astype(np.uint8).reshape(k // 512, 16, n))


def unpack_weight(words, scales, fmt):
    g, p, n, _ = words.shape
    if fmt == "e4m3":
        vals = np.ascontiguousarray(words).view(ml_dtypes.float8_e4m3fn).astype(np.float64)
    else:
        nib = np.empty((g, p, n, 4), np.uint8)
        nib[..., 0::2] = words & 0xF
        nib[..., 1::2] = words >> 4
        vals = E2M1[nib]
    vals = vals * np.repeat(np.exp2(scales.astype(np.float64) - 127.0), 8, axis=1)[..., None]
    return vals.transpose(0, 1, 3, 2).reshape(g * 512, n)


B, C, CP, H, W, KW = 1, 2048, 19, 8, 16, 7
PAD = KW // 2
BN_EPS = 1e-5
FMT = "e4m3"


def pad_hw(v):
    return np.pad(v, ((0, 0), (0, 0), (PAD, PAD), (PAD, PAD)))


def setup_inputs():
    s, t = mx_kscale(C), mx_kscale(C)
    x = bf(np.random.standard_normal((B, C, H, W)))
    coarse_probs = bf(np.random.random((B, CP, H, W)))
    sigma = bf(1.5 + 0.1 * np.random.standard_normal(1))
    w_feat = np.random.standard_normal((C, C)) * 2.0 / np.sqrt(C) * t[:, None] / s[None, :]
    w_fuse = np.random.standard_normal((C, C)) * 2.5 / np.sqrt(C) / t[None, :]
    w_feat_words, w_feat_scales = pack_weight(np.ascontiguousarray(w_feat.T), FMT)
    w_fuse_words, w_fuse_scales = pack_weight(np.ascontiguousarray(w_fuse.T), FMT)
    return {
        "x": x,
        "coarse_probs": coarse_probs,
        "sigma": sigma,
        "w_feat_words": w_feat_words,
        "w_feat_scales": w_feat_scales,
        "w_fuse_words": w_fuse_words,
        "w_fuse_scales": w_fuse_scales,
        "bn_gamma": bf((1.0 + 0.1 * np.random.standard_normal(C)) * s),
        "bn_beta": bf(0.1 * np.random.standard_normal(C) * s),
        "bn_mean": bf(0.1 * np.random.standard_normal(C)),
        "bn_var": bf(np.random.random(C) + 0.5),
    }


def reference(x, coarse_probs, sigma, w_feat_words, w_feat_scales, w_fuse_words, w_fuse_scales, bn_gamma, bn_beta, bn_mean, bn_var):
    x, p = f64(x), f64(coarse_probs)
    inv = 1.0 / np.sqrt(f64(bn_var) + BN_EPS)
    xn = (x - f64(bn_mean)[None, :, None, None]) * (inv * f64(bn_gamma))[None, :, None, None] + f64(bn_beta)[None, :, None, None]

    pp = pad_hw(p)
    dist_sq = np.stack([((pp[:, :, i:i + H, j:j + W] - p) ** 2).sum(axis=1) for i in range(KW) for j in range(KW)], axis=1)
    denom = 2.0 * np.maximum(f64(sigma)[0], 0.0) ** 2 + 1e-8
    a = np.exp(-dist_sq / denom)
    e = np.exp(a - a.max(axis=1, keepdims=True))
    affinity = e / e.sum(axis=1, keepdims=True)

    xq = mxq(xn, 1, "e4m3")
    messages = (unpack_weight(w_feat_words, w_feat_scales, FMT).T @ xq.reshape(B, C, H * W)).reshape(B, C, H, W)

    mp = pad_hw(messages)
    agg = np.zeros((B, C, H, W))
    for i in range(KW):
        for j in range(KW):
            agg = agg + mp[:, :, i:i + H, j:j + W] * affinity[:, i * KW + j][:, None]

    aq = mxq(agg, 1, "e4m3")
    refined = (unpack_weight(w_fuse_words, w_fuse_scales, FMT).T @ aq.reshape(B, C, H * W)).reshape(B, C, H, W)
    return x + refined

@@ -1,0 +1,247 @@
+from contextlib import ExitStack
+
+import concourse.mybir as mybir
+from concourse.masks import make_identity
+
+F32 = mybir.dt.float32
+BF16 = mybir.dt.bfloat16
+I32 = mybir.dt.int32
+U32 = mybir.dt.uint32
+U8 = mybir.dt.uint8
+FP8X4 = mybir.dt.float8_e4m3fn_x4
+ALU = mybir.AluOpType
+ACT = mybir.ActivationFunctionType
+AX = mybir.AxisListType
+
+P = 128
+C = 2048
+G = 4
+T = 4
+CP = 19
+NCH = 512
+BN_EPS = 1e-5
+
+FLOPS = 2 * 2 * C * C * P + 2 * 49 * C * P
+
+
+def tile_dcblock_w_kernel(
+    tc, x, coarse_probs, sigma, w_feat_words, w_feat_scales, w_fuse_words, w_fuse_scales,
+    bn_gamma, bn_beta, bn_mean, bn_var, out,
+):
+    nc = tc.nc
+    with ExitStack() as ctx:
+        keep = ctx.enter_context(tc.tile_pool(name="keep", bufs=1))
+        psum = ctx.enter_context(tc.psum_pool(name="psum", bufs=1))
+
+        def bank(i, shape, dtype, name):
+            return psum.tile(shape, dtype, tag="b%d" % i, name=name)
+
+        wf_words = keep.tile([P, G, C], U32, align_bytes=64)
+        wu_words = keep.tile([P, G, C], U32, align_bytes=64)
+        wf_planes = keep.tile([P, C], U8, align_bytes=64)
+        wu_planes = keep.tile([P, C], U8, align_bytes=64)
+        x_sb = keep.tile([P, G, T, P], BF16)
+        xg = keep.tile([P, G, P, T], BF16, align_bytes=64)
+        xq_words = keep.tile([P, G, P], U32, align_bytes=64)
+        xq_planes = keep.tile([P, G, P], U8, align_bytes=64)
+        ag = keep.tile([P, G, P, T], BF16, align_bytes=64)
+        aq_words = keep.tile([P, G, P], U32, align_bytes=64)
+        aq_planes = keep.tile([P, G, P], U8, align_bytes=64)
+        small = keep.tile([P, 640], BF16)
+        sig = keep.tile([P, 1], BF16)
+        ident_f = keep.tile([P, P], F32)
+        ident_b = keep.tile([P, P], BF16)
+
+        nc.vector.memset(small[:], 0.0)
+        nc.vector.memset(wf_planes[:].bitcast(I32), 0)
+        nc.vector.memset(wu_planes[:].bitcast(I32), 0)
+        warm = keep.tile([P, 1], F32)
+        nc.vector.memset(warm[:], 1.0)
+        nc.scalar.activation(out=warm[:], in_=warm[:], func=ACT.Sqrt)
+
+        for v, vec in enumerate((bn_var, bn_gamma, bn_mean, bn_beta)):
+            nc.scalar.dma_start(out=small[4 * v:4 * v + 4, 0:512], in_=vec.rearrange("(g k) -> g k", g=G))
+        nc.sync.dma_start(
+            out=x_sb[:].rearrange("p g t n -> p g (t n)"),
+            in_=x.rearrange("b (g p t) h w -> p (b g) (t h w)", p=P, t=T),
+        )
+        nc.scalar.dma_start(out=small[0:CP, 512:640], in_=coarse_probs.rearrange("b c h w -> (b c) (h w)"))
+        nc.scalar.dma_start(out=sig[:], in_=sigma.partition_broadcast(P))
+
+        def load_planes(planes, scales):
+            for q in range(4):
+                nc.sync.dma_start(
+                    out=planes[32 * q:32 * q + 16, :].bitcast(I32),
+                    in_=scales[:, 4 * q:4 * q + 4, :].bitcast(I32),
+                )
+
+        def load_words(words, dram, g0, gn, c0, cn):
+            nc.sync.dma_start(
+                out=words[:, g0:g0 + gn, c0:c0 + cn].bitcast(I32),
+                in_=dram.rearrange("g p n t -> p g (n t)")[:, g0:g0 + gn, T * c0:T * (c0 + cn)].bitcast(I32),
+            )
+
+        load_planes(wf_planes, w_feat_scales)
+        load_planes(wu_planes, w_fuse_scales)
+        for piece in ((0, 2, 0, 1024), (2, 2, 0, 1024), (0, 2, 1024, 1024), (2, 1, 1024, 1024),
+                      (3, 1, 1024, 512), (3, 1, 1536, 512)):
+            load_words(wf_words, w_feat_words, *piece)
+        for piece in ((0, 1, 0, C), (1, 1, 0, C), (2, 1, 0, C),
+                      (3, 1, 0, 512), (3, 1, 512, 512), (3, 1, 1024, 512), (3, 1, 1536, 512)):
+            load_words(wu_words, w_fuse_words, *piece)
+
+        make_identity(nc, ident_f[:])
+        nc.vector.tensor_copy(out=ident_b[:], in_=ident_f[:])
+        wcol = keep.tile([P, 8, 16], F32)
+        nc.gpsimd.iota(wcol[:], pattern=[[0, 8], [1, 16]], base=0, channel_multiplier=0,
+                       allow_small_or_imprecise_dtypes=True)
+        dlin = keep.tile([P, P], F32)
+        nc.gpsimd.iota(dlin[:], pattern=[[1, P]], base=0, channel_multiplier=-1,
+                       allow_small_or_imprecise_dtypes=True)
+        pidx = keep.tile([P, 1], I32)
+        nc.gpsimd.iota(pidx[:], pattern=[[0, 1]], base=0, channel_multiplier=1)
+        wrow_i = keep.tile([P, 1], I32)
+        nc.vector.tensor_single_scalar(out=wrow_i[:], in_=pidx[:], scalar=15, op=ALU.bitwise_and)
+        wrow = keep.tile([P, 1], F32)
+        nc.vector.tensor_copy(out=wrow[:], in_=wrow_i[:])
+        dw = keep.tile([P, P], F32)
+        nc.vector.tensor_scalar(out=dw[:], in0=wcol[:].rearrange("p h w -> p (h w)"), scalar1=wrow[:, 0:1],
+                                scalar2=None, op0=ALU.subtract)
+        nc.vector.tensor_tensor(out=dw[:], in0=dw[:], in1=dw[:], op=ALU.mult)
+        nc.vector.tensor_scalar(out=dw[:], in0=dw[:], scalar1=9.5, scalar2=None, op0=ALU.is_le)
+        nc.vector.tensor_tensor(out=dlin[:], in0=dlin[:], in1=dlin[:], op=ALU.mult)
+        nc.vector.tensor_scalar(out=dlin[:], in0=dlin[:], scalar1=2652.25, scalar2=None, op0=ALU.is_le)
+        mask = keep.tile([P, P], F32)
+        nc.vector.tensor_tensor(out=mask[:], in0=dw[:], in1=dlin[:], op=ALU.mult)
+        n_out = keep.tile([P, 1], F32)
+        nc.vector.tensor_reduce(out=n_out[:], in_=mask[:], axis=AX.X, op=ALU.add)
+        nc.vector.tensor_scalar(out=n_out[:], in0=n_out[:], scalar1=-1.0, scalar2=49.0, op0=ALU.mult, op1=ALU.add)
+
+        ps_bn = bank(4, [P, T, P], BF16, "ps_bn")
+        for t in range(T):
+            nc.tensor.transpose(ps_bn[:, t, :], small[:, t:512:T], ident_b[:])
+        bn = keep.tile([P, 4, G * T], F32)
+        nc.vector.tensor_copy(
+            out=bn[:].rearrange("p v (g t) -> p (v g) t", t=T),
+            in_=ps_bn[:, :, 0:16].rearrange("p t r -> p r t"),
+        )
+        ve = keep.tile([P, G * T], F32)
+        rs = keep.tile([P, G * T], F32)
+        nt = keep.tile([P, G * T], F32)
+        sc = keep.tile([P, G * T], F32)
+        bi = keep.tile([P, G * T], F32)
+        nc.vector.tensor_scalar(out=ve[:], in0=bn[:, 0, :], scalar1=BN_EPS, scalar2=None, op0=ALU.add)
+        nc.scalar.activation(out=rs[:], in_=ve[:], func=ACT.Sqrt)
+        nc.vector.reciprocal(out=rs[:], in_=rs[:])
+        nc.vector.tensor_tensor(out=nt[:], in0=rs[:], in1=rs[:], op=ALU.mult)
+        nc.vector.tensor_tensor(out=nt[:], in0=nt[:], in1=ve[:], op=ALU.mult)
+        nc.vector.tensor_scalar(out=nt[:], in0=nt[:], scalar1=-0.5, scalar2=1.5, op0=ALU.mult, op1=ALU.add)
+        nc.vector.tensor_tensor(out=rs[:], in0=rs[:], in1=nt[:], op=ALU.mult)
+        nc.vector.tensor_tensor(out=sc[:], in0=rs[:], in1=bn[:, 1, :], op=ALU.mult)
+        nc.vector.tensor_tensor(out=nt[:], in0=sc[:], in1=bn[:, 2, :], op=ALU.mult)
+        nc.vector.tensor_tensor(out=bi[:], in0=bn[:, 3, :], in1=nt[:], op=ALU.subtract)
+
+        for g in range(G):
+            for t in range(T):
+                k = g * T + t
+                if g < 2:
+                    nc.vector.tensor_scalar(out=xg[:, g, :, t], in0=x_sb[:, g, t, :], scalar1=sc[:, k:k + 1],
+                                            scalar2=bi[:, k:k + 1], op0=ALU.mult, op1=ALU.add)
+                else:
+                    nc.scalar.activation(out=xg[:, g, :, t], in_=x_sb[:, g, t, :], func=ACT.Identity,
+                                         bias=bi[:, k:k + 1], scale=sc[:, k:k + 1])
+        for g in range(G):
+            nc.vector.quantize_mx(
+                out=xq_words[:, g, :].bitcast(FP8X4), scales=xq_planes[:, g, :],
+                in_=xg[:, g, :, :].rearrange("p n t -> p (n t)"),
+            )
+
+        ps_pt = bank(5, [P, P], BF16, "ps_pt")
+        nc.tensor.transpose(ps_pt[:], small[:, 512:640], ident_b[:])
+        pT = keep.tile([P, CP], F32)
+        nc.vector.tensor_copy(out=pT[:], in_=ps_pt[:, 0:CP])
+        dist = keep.tile([P, 136], F32)
+        junk = keep.tile([P, CP], F32)
+        nc.scalar.activation(out=junk[:], in_=pT[:], func=ACT.Square, accum_out=dist[:, 128:129])
+        sq = keep.tile([P, CP, P], F32)
+        for j, (c0, cn) in enumerate(((0, 8), (8, 8), (16, 3))):
+            ps_bc = bank(j, [P, 8, P], BF16, "ps_bc%d" % j)
+            for c in range(cn):
+                nc.tensor.matmul(ps_bc[:, c, :], lhsT=ident_b[:, c0 + c:c0 + c + 1].to_broadcast([P, P]),
+                                 rhs=small[:, 512:640], start=True, stop=True)
+            nc.vector.tensor_tensor(out=sq[:, c0:c0 + cn, :], in0=ps_bc[:, 0:cn, :],
+                                    in1=pT[:, c0:c0 + cn].unsqueeze(2).to_broadcast([P, cn, P]), op=ALU.subtract)
+            nc.scalar.activation(out=sq[:, c0:c0 + cn, :], in_=sq[:, c0:c0 + cn, :], func=ACT.Square)
+        s8 = keep.tile([P, 8, P], F32)
+        nc.vector.tensor_tensor(out=s8[:], in0=sq[:, 0:8, :], in1=sq[:, 8:16, :], op=ALU.add)
+        nc.vector.tensor_tensor(out=s8[:, 0:4, :], in0=s8[:, 0:4, :], in1=s8[:, 4:8, :], op=ALU.add)
+        nc.vector.tensor_tensor(out=s8[:, 0:3, :], in0=s8[:, 0:3, :], in1=sq[:, 16:19, :], op=ALU.add)
+        nc.vector.tensor_tensor(out=s8[:, 0:2, :], in0=s8[:, 0:2, :], in1=s8[:, 2:4, :], op=ALU.add)
+        nc.vector.tensor_tensor(out=dist[:, 0:P], in0=s8[:, 0, :], in1=s8[:, 1, :], op=ALU.add)
+
+        den = keep.tile([P, 1], F32)
+        nc.vector.tensor_scalar(out=den[:], in0=sig[:], scalar1=0.0, scalar2=None, op0=ALU.max)
+        nc.vector.tensor_tensor(out=den[:], in0=den[:], in1=den[:], op=ALU.mult)
+        nc.vector.tensor_scalar(out=den[:], in0=den[:], scalar1=2.0, scalar2=1e-8, op0=ALU.mult, op1=ALU.add)
+        nc.vector.reciprocal(out=den[:], in_=den[:])
+        nc.vector.tensor_scalar(out=den[:], in0=den[:], scalar1=-1.0, scalar2=None, op0=ALU.mult)
+
+        ex = keep.tile([P, 136], F32)
+        nc.scalar.activation(out=ex[:, 0:129], in_=dist[:, 0:129], func=ACT.Exp, scale=den[:, 0:1])
+        nc.scalar.activation(out=ex[:, 0:129], in_=ex[:, 0:129], func=ACT.Exp, bias=-1.0)
+        at = keep.tile([P, P], F32)
+        ssum = keep.tile([P, 1], F32)
+        nc.vector.tensor_tensor(out=at[:], in0=ex[:, 0:P], in1=mask[:], op=ALU.mult)
+        nc.vector.tensor_reduce(out=ssum[:], in_=at[:], axis=AX.X, op=ALU.add)
+        nc.vector.tensor_scalar(out=ssum[:], in0=ex[:, 128:129], scalar1=n_out[:, 0:1], scalar2=ssum[:, 0:1],
+                                op0=ALU.mult, op1=ALU.add)
+        nc.vector.reciprocal(out=ssum[:], in_=ssum[:])
+        nc.vector.tensor_scalar(out=at[:], in0=at[:], scalar1=ssum[:, 0:1], scalar2=None, op0=ALU.mult)
+        ps_aff = bank(3, [P, P], F32, "ps_aff")
+        nc.tensor.transpose(ps_aff[:], at[:], ident_f[:])
+        aff = keep.tile([P, P], F32)
+        nc.vector.tensor_copy(out=aff[:], in_=ps_aff[:])
+
+        ps_m = [bank(4 + c, [P, NCH], F32, "ps_m%d" % c) for c in range(G)]
+        for half in range(2):
+            for g in range(G):
+                for c in (2 * half, 2 * half + 1):
+                    cols = slice(c * NCH, (c + 1) * NCH)
+                    nc.tensor.matmul_mx(
+                        out=ps_m[c][:], lhsT=xq_words[:, g, :].bitcast(FP8X4), lhsT_scale=xq_planes[:, g, :],
+                        rhs=wf_words[:, g, cols].bitcast(FP8X4), rhs_scale=wf_planes[4 * g:P, cols],
+                        start=(g == 0), stop=(g == G - 1),
+                    )
+
+        mt = keep.tile([P, G, T, P], F32)
+        for c in range(G):
+            nc.scalar.copy(out=mt[:, c, :, :], in_=ps_m[c][:].rearrange("q (p t) -> q t p", t=T))
+            ps_a = bank(4 + c, [P, T, P], F32, "ps_a%d" % c)
+            for t in range(T):
+                nc.tensor.matmul(ps_a[:, t, :], lhsT=mt[:, c, t, :], rhs=aff[:], start=True, stop=True)
+            nc.vector.tensor_copy(out=ag[:, c, :, :], in_=ps_a[:].rearrange("p t n -> p n t"))
+            nc.vector.quantize_mx(
+                out=aq_words[:, c, :].bitcast(FP8X4), scales=aq_planes[:, c, :],
+                in_=ag[:, c, :, :].rearrange("p n t -> p (n t)"),
+            )
+
+        ps_r = [bank(c, [P, NCH], F32, "ps_r%d" % c) for c in range(G)]
+        for g in range(G):
+            for c in range(G):
+                cols = slice(c * NCH, (c + 1) * NCH)
+                nc.tensor.matmul_mx(
+                    out=ps_r[c][:], lhsT=aq_words[:, g, :].bitcast(FP8X4), lhsT_scale=aq_planes[:, g, :],
+                    rhs=wu_words[:, g, cols].bitcast(FP8X4), rhs_scale=wu_planes[4 * g:P, cols],
+                    start=(g == 0), stop=(g == G - 1),
+                )
+
+        rt = keep.tile([P, G, T, P], F32)
+        o_sb = keep.tile([P, G, T, P], F32)
+        out_v = out.rearrange("b (g p t) h w -> p (b g) (t h w)", p=P, t=T)
+        for c in range(G):
+            nc.scalar.copy(out=rt[:, c, :, :], in_=ps_r[c][:].rearrange("q (p t) -> q t p", t=T))
+            ps_o = bank(4 + c, [P, T, P], F32, "ps_o%d" % c)
+            for t in range(T):
+                nc.tensor.transpose(ps_o[:, t, :], rt[:, c, t, :], ident_f[:])
+            nc.vector.tensor_tensor(out=o_sb[:, c, :, :], in0=ps_o[:], in1=x_sb[:, c, :, :], op=ALU.add)
+            nc.sync.dma_start(out=out_v[:, c, :], in_=o_sb[:, c, :, :].rearrange("p t n -> p (t n)"))

@@ -19,7 +19,12 @@ G = 4
 T = 4
 CP = 19
 NCH = 512
+HALF = 1024
 BN_EPS = 1e-5
+
+ZCOL = CP * P
+SCOL = 2464
+DCOLS = 2496
 
 FLOPS = 2 * 2 * C * C * P + 2 * 49 * C * P
 
@@ -30,6 +35,7 @@ def tile_dcblock_w_kernel(
 ):
     nc = tc.nc
     with ExitStack() as ctx:
+        ctx.enter_context(tc.manual_schedule())
         keep = ctx.enter_context(tc.tile_pool(name="keep", bufs=1))
         psum = ctx.enter_context(tc.psum_pool(name="psum", bufs=1))
 
@@ -40,33 +46,20 @@ def tile_dcblock_w_kernel(
         wu_words = keep.tile([P, G, C], U32, align_bytes=64)
         wf_planes = keep.tile([P, C], U8, align_bytes=64)
         wu_planes = keep.tile([P, C], U8, align_bytes=64)
-        x_sb = keep.tile([P, G, T, P], BF16)
+        x_sb = keep.tile([P, G, T, P], BF16, align_bytes=64)
+        xn = keep.tile([P, G, T, P], BF16, align_bytes=64)
         xg = keep.tile([P, G, P, T], BF16, align_bytes=64)
         xq_words = keep.tile([P, G, P], U32, align_bytes=64)
         xq_planes = keep.tile([P, G, P], U8, align_bytes=64)
         ag = keep.tile([P, G, P, T], BF16, align_bytes=64)
         aq_words = keep.tile([P, G, P], U32, align_bytes=64)
         aq_planes = keep.tile([P, G, P], U8, align_bytes=64)
-        small = keep.tile([P, 640], BF16)
-        sig = keep.tile([P, 1], BF16)
-        ident_f = keep.tile([P, P], F32)
-        ident_b = keep.tile([P, P], BF16)
-
-        nc.vector.memset(small[:], 0.0)
-        nc.vector.memset(wf_planes[:].bitcast(I32), 0)
-        nc.vector.memset(wu_planes[:].bitcast(I32), 0)
-        warm = keep.tile([P, 1], F32)
-        nc.vector.memset(warm[:], 1.0)
-        nc.scalar.activation(out=warm[:], in_=warm[:], func=ACT.Sqrt)
-
-        for v, vec in enumerate((bn_var, bn_gamma, bn_mean, bn_beta)):
-            nc.scalar.dma_start(out=small[4 * v:4 * v + 4, 0:512], in_=vec.rearrange("(g k) -> g k", g=G))
-        nc.sync.dma_start(
-            out=x_sb[:].rearrange("p g t n -> p g (t n)"),
-            in_=x.rearrange("b (g p t) h w -> p (b g) (t h w)", p=P, t=T),
-        )
-        nc.scalar.dma_start(out=small[0:CP, 512:640], in_=coarse_probs.rearrange("b c h w -> (b c) (h w)"))
-        nc.scalar.dma_start(out=sig[:], in_=sigma.partition_broadcast(P))
+        small = keep.tile([P, 512], BF16, align_bytes=64)
+        dl = keep.tile([P, P], BF16, align_bytes=64)
+        dr = keep.tile([P, DCOLS], BF16, align_bytes=64)
+        ident_b = keep.tile([P, P], BF16, align_bytes=64)
+        ident_f = keep.tile([P, P], F32, align_bytes=64)
+        ident_2 = keep.tile([P, 32, 2], BF16, align_bytes=64)
 
         def load_planes(planes, scales):
             for q in range(4):
@@ -81,43 +74,65 @@ def tile_dcblock_w_kernel(
                 in_=dram.rearrange("g p n t -> p g (n t)")[:, g0:g0 + gn, T * c0:T * (c0 + cn)].bitcast(I32),
             )
 
+        nc.gpsimd.memset(small[:].bitcast(I32), 0)
+        make_identity(nc, ident_b[:])
+        for v, vec in enumerate((bn_var, bn_gamma, bn_mean, bn_beta)):
+            nc.sync.dma_start(out=small[4 * v:4 * v + 4, :], in_=vec.rearrange("(g k) -> g k", g=G))
+        nc.vector.memset(dl[:], -1.0)
+        nc.gpsimd.dma_start(out=dl[0:CP, :], in_=coarse_probs.rearrange("b c h w -> (b c) (h w)"))
+        nc.sync.dma_start(
+            out=x_sb[:].rearrange("p g t n -> p g (t n)"),
+            in_=x.rearrange("b (g p t) h w -> p (b g) (t h w)", p=P, t=T),
+        )
+        nc.vector.memset(dr[:, ZCOL:DCOLS], 0.0)
+        nc.scalar.dma_start(out=dr[32:33, SCOL:SCOL + 1], in_=sigma.unsqueeze(0))
+        warm = keep.tile([P, 1], F32)
+        nc.vector.memset(warm[:], 1.0)
+        nc.scalar.activation(out=warm[:], in_=warm[:], func=ACT.Sqrt)
+        nc.vector.tensor_copy(out=ident_2[:], in_=ident_b[:, 0:32].unsqueeze(2).to_broadcast([P, 32, 2]))
+        nc.vector.tensor_copy(
+            out=dr[:, 0:CP * P].bitcast(F32).rearrange("p (c n) -> p c n", c=CP),
+            in_=ident_2[:].rearrange("p c i -> p (c i)").bitcast(F32)[:, 0:CP].unsqueeze(2).to_broadcast([P, CP, P // 2]),
+        )
+        nc.sync.dma_start(out=dr[32:33, 0:CP * P], in_=coarse_probs.rearrange("b c h w -> b (c h w)"))
+        load_words(wf_words, w_feat_words, 0, 1, 0, HALF)
+        nc.vector.tensor_copy(out=dr[0:32, ZCOL:ZCOL + CP], in_=ident_b[0:32, 0:CP])
+        nc.vector.memset(wf_planes[:].bitcast(I32), 0)
         load_planes(wf_planes, w_feat_scales)
+        load_words(wf_words, w_feat_words, 1, 1, 0, HALF)
+        load_words(wf_words, w_feat_words, 2, 2, 0, HALF)
+        load_words(wf_words, w_feat_words, 0, 2, HALF, HALF)
+        load_words(wf_words, w_feat_words, 2, 2, HALF, HALF)
+        nc.vector.tensor_copy(out=ident_f[:], in_=ident_b[:])
+        nc.vector.memset(wu_planes[:].bitcast(I32), 0)
         load_planes(wu_planes, w_fuse_scales)
-        for piece in ((0, 2, 0, 1024), (2, 2, 0, 1024), (0, 2, 1024, 1024), (2, 1, 1024, 1024),
-                      (3, 1, 1024, 512), (3, 1, 1536, 512)):
-            load_words(wf_words, w_feat_words, *piece)
-        for piece in ((0, 1, 0, C), (1, 1, 0, C), (2, 1, 0, C),
-                      (3, 1, 0, 512), (3, 1, 512, 512), (3, 1, 1024, 512), (3, 1, 1536, 512)):
+        for piece in ((0, 2, 0, HALF), (2, 2, 0, HALF), (0, 2, HALF, HALF), (2, 1, HALF, HALF),
+                      (3, 1, HALF, NCH), (3, 1, HALF + NCH, NCH)):
             load_words(wu_words, w_fuse_words, *piece)
 
-        make_identity(nc, ident_f[:])
-        nc.vector.tensor_copy(out=ident_b[:], in_=ident_f[:])
+        pidx = keep.tile([P, 1], I32)
+        nc.gpsimd.iota(pidx[:], pattern=[[0, 1]], base=0, channel_multiplier=1)
         wcol = keep.tile([P, 8, 16], F32)
         nc.gpsimd.iota(wcol[:], pattern=[[0, 8], [1, 16]], base=0, channel_multiplier=0,
                        allow_small_or_imprecise_dtypes=True)
         dlin = keep.tile([P, P], F32)
         nc.gpsimd.iota(dlin[:], pattern=[[1, P]], base=0, channel_multiplier=-1,
                        allow_small_or_imprecise_dtypes=True)
-        pidx = keep.tile([P, 1], I32)
-        nc.gpsimd.iota(pidx[:], pattern=[[0, 1]], base=0, channel_multiplier=1)
         wrow_i = keep.tile([P, 1], I32)
         nc.vector.tensor_single_scalar(out=wrow_i[:], in_=pidx[:], scalar=15, op=ALU.bitwise_and)
         wrow = keep.tile([P, 1], F32)
         nc.vector.tensor_copy(out=wrow[:], in_=wrow_i[:])
         dw = keep.tile([P, P], F32)
-        nc.vector.tensor_scalar(out=dw[:], in0=wcol[:].rearrange("p h w -> p (h w)"), scalar1=wrow[:, 0:1],
-                                scalar2=None, op0=ALU.subtract)
-        nc.vector.tensor_tensor(out=dw[:], in0=dw[:], in1=dw[:], op=ALU.mult)
-        nc.vector.tensor_scalar(out=dw[:], in0=dw[:], scalar1=9.5, scalar2=None, op0=ALU.is_le)
-        nc.vector.tensor_tensor(out=dlin[:], in0=dlin[:], in1=dlin[:], op=ALU.mult)
-        nc.vector.tensor_scalar(out=dlin[:], in0=dlin[:], scalar1=2652.25, scalar2=None, op0=ALU.is_le)
         mask = keep.tile([P, P], F32)
-        nc.vector.tensor_tensor(out=mask[:], in0=dw[:], in1=dlin[:], op=ALU.mult)
-        n_out = keep.tile([P, 1], F32)
-        nc.vector.tensor_reduce(out=n_out[:], in_=mask[:], axis=AX.X, op=ALU.add)
-        nc.vector.tensor_scalar(out=n_out[:], in0=n_out[:], scalar1=-1.0, scalar2=49.0, op0=ALU.mult, op1=ALU.add)
+        nc.gpsimd.tensor_tensor(out=dlin[:], in0=dlin[:], in1=dlin[:], op=ALU.mult)
+        nc.gpsimd.tensor_scalar(out=dlin[:], in0=dlin[:], scalar1=2652.25, scalar2=None, op0=ALU.is_le)
+        nc.gpsimd.tensor_scalar(out=dw[:], in0=wcol[:].rearrange("p h w -> p (h w)"), scalar1=wrow[:, 0:1],
+                                scalar2=None, op0=ALU.subtract)
+        nc.gpsimd.tensor_tensor(out=dw[:], in0=dw[:], in1=dw[:], op=ALU.mult)
+        nc.gpsimd.tensor_scalar(out=dw[:], in0=dw[:], scalar1=9.5, scalar2=None, op0=ALU.is_le)
+        nc.gpsimd.tensor_tensor(out=mask[:], in0=dw[:], in1=dlin[:], op=ALU.mult)
 
-        ps_bn = bank(4, [P, T, P], BF16, "ps_bn")
+        ps_bn = bank(6, [P, T, P], BF16, "ps_bn")
         for t in range(T):
             nc.tensor.transpose(ps_bn[:, t, :], small[:, t:512:T], ident_b[:])
         bn = keep.tile([P, 4, G * T], F32)
@@ -132,80 +147,72 @@ def tile_dcblock_w_kernel(
         bi = keep.tile([P, G * T], F32)
         nc.vector.tensor_scalar(out=ve[:], in0=bn[:, 0, :], scalar1=BN_EPS, scalar2=None, op0=ALU.add)
         nc.scalar.activation(out=rs[:], in_=ve[:], func=ACT.Sqrt)
+        nc.scalar.activation(out=warm[:], in_=warm[:], func=ACT.Exp)
         nc.vector.reciprocal(out=rs[:], in_=rs[:])
-        nc.vector.tensor_tensor(out=nt[:], in0=rs[:], in1=rs[:], op=ALU.mult)
-        nc.vector.tensor_tensor(out=nt[:], in0=nt[:], in1=ve[:], op=ALU.mult)
-        nc.vector.tensor_scalar(out=nt[:], in0=nt[:], scalar1=-0.5, scalar2=1.5, op0=ALU.mult, op1=ALU.add)
-        nc.vector.tensor_tensor(out=rs[:], in0=rs[:], in1=nt[:], op=ALU.mult)
         nc.vector.tensor_tensor(out=sc[:], in0=rs[:], in1=bn[:, 1, :], op=ALU.mult)
         nc.vector.tensor_tensor(out=nt[:], in0=sc[:], in1=bn[:, 2, :], op=ALU.mult)
         nc.vector.tensor_tensor(out=bi[:], in0=bn[:, 3, :], in1=nt[:], op=ALU.subtract)
 
-        for g in range(G):
+        ps_d = [bank(j, [P, NCH], F32, "ps_d%d" % j) for j in range(5)]
+        for j in range(5):
+            c0, c1 = j * NCH, min((j + 1) * NCH, DCOLS)
+            nc.tensor.matmul(ps_d[j][:, 0:c1 - c0], lhsT=dl[:], rhs=dr[:, c0:c1], start=True, stop=True)
+        sq = keep.tile([P, CP * P], F32)
+        dist0 = keep.tile([P, 1], F32)
+        junk = keep.tile([P, CP], F32)
+        for j in range(5):
+            c0, c1 = j * NCH, min((j + 1) * NCH, CP * P)
+            nc.scalar.activation(out=sq[:, c0:c1], in_=ps_d[j][:, 0:c1 - c0], func=ACT.Square)
+        nc.scalar.activation(out=junk[:], in_=ps_d[4][:, ZCOL - 2048:ZCOL - 2048 + CP], func=ACT.Square,
+                             accum_out=dist0[:])
+        ps_dist = bank(5, [P, P], F32, "ps_dist")
+
+        def add_squares(cs):
+            for c in cs:
+                nc.tensor.matmul(ps_dist[:], lhsT=sq[:, c * P:(c + 1) * P], rhs=ident_f[:], is_transpose=True,
+                                 start=(c == 0), stop=(c == CP - 1))
+
+        def bn_apply(g):
             for t in range(T):
                 k = g * T + t
-                if g < 2:
-                    nc.vector.tensor_scalar(out=xg[:, g, :, t], in0=x_sb[:, g, t, :], scalar1=sc[:, k:k + 1],
-                                            scalar2=bi[:, k:k + 1], op0=ALU.mult, op1=ALU.add)
-                else:
-                    nc.scalar.activation(out=xg[:, g, :, t], in_=x_sb[:, g, t, :], func=ACT.Identity,
-                                         bias=bi[:, k:k + 1], scale=sc[:, k:k + 1])
-        for g in range(G):
+                nc.vector.tensor_scalar(out=xn[:, g, t, :], in0=x_sb[:, g, t, :], scalar1=sc[:, k:k + 1],
+                                        scalar2=bi[:, k:k + 1], op0=ALU.mult, op1=ALU.add)
+
+        def regroup(g):
+            nc.vector.tensor_copy(out=xg[:, g, :, :], in_=xn[:, g, :, :].rearrange("p t n -> p n t"))
+
+        def quantise_x(g):
             nc.vector.quantize_mx(
                 out=xq_words[:, g, :].bitcast(FP8X4), scales=xq_planes[:, g, :],
                 in_=xg[:, g, :, :].rearrange("p n t -> p (n t)"),
             )
 
-        ps_pt = bank(5, [P, P], BF16, "ps_pt")
-        nc.tensor.transpose(ps_pt[:], small[:, 512:640], ident_b[:])
-        pT = keep.tile([P, CP], F32)
-        nc.vector.tensor_copy(out=pT[:], in_=ps_pt[:, 0:CP])
-        dist = keep.tile([P, 136], F32)
-        junk = keep.tile([P, CP], F32)
-        nc.scalar.activation(out=junk[:], in_=pT[:], func=ACT.Square, accum_out=dist[:, 128:129])
-        sq = keep.tile([P, CP, P], F32)
-        for j, (c0, cn) in enumerate(((0, 8), (8, 8), (16, 3))):
-            ps_bc = bank(j, [P, 8, P], BF16, "ps_bc%d" % j)
-            for c in range(cn):
-                nc.tensor.matmul(ps_bc[:, c, :], lhsT=ident_b[:, c0 + c:c0 + c + 1].to_broadcast([P, P]),
-                                 rhs=small[:, 512:640], start=True, stop=True)
-            nc.vector.tensor_tensor(out=sq[:, c0:c0 + cn, :], in0=ps_bc[:, 0:cn, :],
-                                    in1=pT[:, c0:c0 + cn].unsqueeze(2).to_broadcast([P, cn, P]), op=ALU.subtract)
-            nc.scalar.activation(out=sq[:, c0:c0 + cn, :], in_=sq[:, c0:c0 + cn, :], func=ACT.Square)
-        s8 = keep.tile([P, 8, P], F32)
-        nc.vector.tensor_tensor(out=s8[:], in0=sq[:, 0:8, :], in1=sq[:, 8:16, :], op=ALU.add)
-        nc.vector.tensor_tensor(out=s8[:, 0:4, :], in0=s8[:, 0:4, :], in1=s8[:, 4:8, :], op=ALU.add)
-        nc.vector.tensor_tensor(out=s8[:, 0:3, :], in0=s8[:, 0:3, :], in1=sq[:, 16:19, :], op=ALU.add)
-        nc.vector.tensor_tensor(out=s8[:, 0:2, :], in0=s8[:, 0:2, :], in1=s8[:, 2:4, :], op=ALU.add)
-        nc.vector.tensor_tensor(out=dist[:, 0:P], in0=s8[:, 0, :], in1=s8[:, 1, :], op=ALU.add)
-
+        bn_apply(0)
+        bn_apply(1)
+        regroup(0)
+        bn_apply(2)
+        quantise_x(0)
+        regroup(1)
+        bn_apply(3)
+        quantise_x(1)
+        regroup(2)
         den = keep.tile([P, 1], F32)
-        nc.vector.tensor_scalar(out=den[:], in0=sig[:], scalar1=0.0, scalar2=None, op0=ALU.max)
+        nc.vector.tensor_scalar(out=den[:], in0=ps_d[4][:, SCOL - 2048:SCOL - 2047], scalar1=-1.0, scalar2=0.0,
+                                op0=ALU.mult, op1=ALU.max)
         nc.vector.tensor_tensor(out=den[:], in0=den[:], in1=den[:], op=ALU.mult)
-        nc.vector.tensor_scalar(out=den[:], in0=den[:], scalar1=2.0, scalar2=1e-8, op0=ALU.mult, op1=ALU.add)
+        regroup(3)
+        nc.vector.tensor_scalar(out=den[:], in0=den[:], scalar1=-2.0, scalar2=-1e-8, op0=ALU.mult, op1=ALU.add)
+        quantise_x(2)
         nc.vector.reciprocal(out=den[:], in_=den[:])
-        nc.vector.tensor_scalar(out=den[:], in0=den[:], scalar1=-1.0, scalar2=None, op0=ALU.mult)
+        quantise_x(3)
 
-        ex = keep.tile([P, 136], F32)
-        nc.scalar.activation(out=ex[:, 0:129], in_=dist[:, 0:129], func=ACT.Exp, scale=den[:, 0:1])
-        nc.scalar.activation(out=ex[:, 0:129], in_=ex[:, 0:129], func=ACT.Exp, bias=-1.0)
-        at = keep.tile([P, P], F32)
-        ssum = keep.tile([P, 1], F32)
-        nc.vector.tensor_tensor(out=at[:], in0=ex[:, 0:P], in1=mask[:], op=ALU.mult)
-        nc.vector.tensor_reduce(out=ssum[:], in_=at[:], axis=AX.X, op=ALU.add)
-        nc.vector.tensor_scalar(out=ssum[:], in0=ex[:, 128:129], scalar1=n_out[:, 0:1], scalar2=ssum[:, 0:1],
-                                op0=ALU.mult, op1=ALU.add)
-        nc.vector.reciprocal(out=ssum[:], in_=ssum[:])
-        nc.vector.tensor_scalar(out=at[:], in0=at[:], scalar1=ssum[:, 0:1], scalar2=None, op0=ALU.mult)
-        ps_aff = bank(3, [P, P], F32, "ps_aff")
-        nc.tensor.transpose(ps_aff[:], at[:], ident_f[:])
-        aff = keep.tile([P, P], F32)
-        nc.vector.tensor_copy(out=aff[:], in_=ps_aff[:])
+        mt = keep.tile([P, G, T, P], F32)
+        m_bank = (6, 7, 0, 1)
+        ps_m = [bank(m_bank[c], [P, NCH], F32, "ps_m%d" % c) for c in range(G)]
 
-        ps_m = [bank(4 + c, [P, NCH], F32, "ps_m%d" % c) for c in range(G)]
-        for half in range(2):
-            for g in range(G):
-                for c in (2 * half, 2 * half + 1):
+        def messages(gs, cs):
+            for g in gs:
+                for c in cs:
                     cols = slice(c * NCH, (c + 1) * NCH)
                     nc.tensor.matmul_mx(
                         out=ps_m[c][:], lhsT=xq_words[:, g, :].bitcast(FP8X4), lhsT_scale=xq_planes[:, g, :],
@@ -213,35 +220,101 @@ def tile_dcblock_w_kernel(
                         start=(g == 0), stop=(g == G - 1),
                     )
 
-        mt = keep.tile([P, G, T, P], F32)
-        for c in range(G):
+        def messages_out(c):
             nc.scalar.copy(out=mt[:, c, :, :], in_=ps_m[c][:].rearrange("q (p t) -> q t p", t=T))
-            ps_a = bank(4 + c, [P, T, P], F32, "ps_a%d" % c)
+
+        def aggregate(c):
+            ps_a = bank(2 + c, [P, T, P], F32, "ps_a%d" % c)
             for t in range(T):
                 nc.tensor.matmul(ps_a[:, t, :], lhsT=mt[:, c, t, :], rhs=aff[:], start=True, stop=True)
-            nc.vector.tensor_copy(out=ag[:, c, :, :], in_=ps_a[:].rearrange("p t n -> p n t"))
+            nc.vector.tensor_tensor(out=ag[:, c, :, :], in0=ps_a[:].rearrange("p t n -> p n t"),
+                                    in1=rsum[:].unsqueeze(2).to_broadcast([P, P, T]), op=ALU.mult)
+
+        def quantise_agg(c):
             nc.vector.quantize_mx(
                 out=aq_words[:, c, :].bitcast(FP8X4), scales=aq_planes[:, c, :],
                 in_=ag[:, c, :, :].rearrange("p n t -> p (n t)"),
             )
 
-        ps_r = [bank(c, [P, NCH], F32, "ps_r%d" % c) for c in range(G)]
-        for g in range(G):
-            for c in range(G):
-                cols = slice(c * NCH, (c + 1) * NCH)
+        add_squares(range(CP))
+        messages(range(G), (0, 1))
+        messages((0, 1), (2, 3))
+
+        ex = keep.tile([P, 136], F32)
+        nc.scalar.activation(out=ex[:, 128:129], in_=dist0[:], func=ACT.Exp, scale=den[:, 0:1])
+        nc.scalar.activation(out=ex[:, 0:128], in_=ps_dist[:], func=ACT.Exp, scale=den[:, 0:1])
+        nc.scalar.activation(out=ex[:, 0:129], in_=ex[:, 0:129], func=ACT.Exp, bias=-1.0)
+        n_out = keep.tile([P, 1], F32)
+        nc.vector.tensor_reduce(out=n_out[:], in_=mask[:], axis=AX.X, op=ALU.add)
+        nc.vector.tensor_scalar(out=n_out[:], in0=n_out[:], scalar1=-1.0, scalar2=49.0, op0=ALU.mult, op1=ALU.add)
+        aff = keep.tile([P, P], F32)
+        own = keep.tile([P, 1], F32)
+        aff_s = keep.tile([P, P], F32)
+        ones = keep.tile([P, P], F32)
+        rsum = keep.tile([P, P], F32)
+        nc.vector.memset(ones[:], 1.0)
+        nc.vector.tensor_tensor(out=aff[:], in0=ex[:, 0:P], in1=mask[:], op=ALU.mult)
+        nc.vector.tensor_tensor(out=own[:], in0=ex[:, 128:129], in1=n_out[:], op=ALU.mult)
+        nc.vector.scalar_tensor_tensor(out=aff_s[:], in0=ident_f[:], scalar=own[:, 0:1], in1=aff[:],
+                                       op0=ALU.mult, op1=ALU.add)
+        ps_s = bank(5, [P, P], F32, "ps_s")
+        nc.tensor.matmul(ps_s[:], lhsT=ones[:], rhs=aff_s[:], start=True, stop=True)
+        nc.vector.reciprocal(out=rsum[:], in_=ps_s[:])
+        messages_out(0)
+        messages_out(1)
+        aggregate(0)
+        aggregate(1)
+        quantise_agg(0)
+        messages((2, 3), (2, 3))
+        messages_out(2)
+        messages_out(3)
+        quantise_agg(1)
+        aggregate(2)
+        aggregate(3)
+        quantise_agg(2)
+        quantise_agg(3)
+
+        rt = keep.tile([P, G, T, P], F32)
+        o_sb = keep.tile([P, G, T, P], F32)
+        out_v = out.rearrange("b (g p t) h w -> p (b g) (t h w)", p=P, t=T)
+        ps_r = [bank(m_bank[c], [P, NCH], F32, "ps_r%d" % c) for c in range(G)]
+
+        def refine(c, gs):
+            cols = slice(c * NCH, (c + 1) * NCH)
+            for g in gs:
                 nc.tensor.matmul_mx(
                     out=ps_r[c][:], lhsT=aq_words[:, g, :].bitcast(FP8X4), lhsT_scale=aq_planes[:, g, :],
                     rhs=wu_words[:, g, cols].bitcast(FP8X4), rhs_scale=wu_planes[4 * g:P, cols],
                     start=(g == 0), stop=(g == G - 1),
                 )
 
-        rt = keep.tile([P, G, T, P], F32)
-        o_sb = keep.tile([P, G, T, P], F32)
-        out_v = out.rearrange("b (g p t) h w -> p (b g) (t h w)", p=P, t=T)
-        for c in range(G):
-            nc.scalar.copy(out=rt[:, c, :, :], in_=ps_r[c][:].rearrange("q (p t) -> q t p", t=T))
-            ps_o = bank(4 + c, [P, T, P], F32, "ps_o%d" % c)
+        def refined_out(c):
+            src = ps_r[c][:].rearrange("q (p t) -> q t p", t=T)
+            nc.scalar.copy(out=rt[:, c, 0:2, :], in_=src[:, 0:2, :])
+            nc.vector.tensor_copy(out=rt[:, c, 2:4, :], in_=src[:, 2:4, :])
+
+        def finish(c, eng):
+            ps_o = bank(2 + c, [P, T, P], F32, "ps_o%d" % c)
             for t in range(T):
                 nc.tensor.transpose(ps_o[:, t, :], rt[:, c, t, :], ident_f[:])
             nc.vector.tensor_tensor(out=o_sb[:, c, :, :], in0=ps_o[:], in1=x_sb[:, c, :, :], op=ALU.add)
-            nc.sync.dma_start(out=out_v[:, c, :], in_=o_sb[:, c, :, :].rearrange("p t n -> p (t n)"))
+            eng.dma_start(out=out_v[:, c, :], in_=o_sb[:, c, :, :].rearrange("p t n -> p (t n)"))
+
+        refine(0, (0, 1))
+        refine(1, (0, 1))
+        refine(0, (2, 3))
+        refined_out(0)
+        refine(1, (2, 3))
+        refined_out(1)
+        finish(0, nc.scalar)
+        refine(2, (0,))
+        refine(3, (0,))
+        finish(1, nc.scalar)
+        refine(2, (1, 2))
+        refine(3, (1, 2))
+        refine(2, (3,))
+        refined_out(2)
+        refine(3, (3,))
+        refined_out(3)
+        finish(2, nc.sync)
+        finish(3, nc.sync)

@@ -22,9 +22,11 @@ NCH = 512
 HALF = 1024
 BN_EPS = 1e-5
 
-ZCOL = CP * P
-SCOL = 2464
-DCOLS = 2496
+ROWS = 4
+KD = ROWS * (CP + 1)
+SIGR = 96
+OUTC = P
+SIGC = P + 2
 
 FLOPS = 2 * 2 * C * C * P + 2 * 49 * C * P
 
@@ -55,11 +57,14 @@ def tile_dcblock_w_kernel(
         aq_words = keep.tile([P, G, P], U32, align_bytes=64)
         aq_planes = keep.tile([P, G, P], U8, align_bytes=64)
         small = keep.tile([P, 512], BF16, align_bytes=64)
-        dl = keep.tile([P, P], BF16, align_bytes=64)
-        dr = keep.tile([P, DCOLS], BF16, align_bytes=64)
+        p4 = keep.tile([P, P], BF16, align_bytes=64)
+        sq = keep.tile([P, P], F32)
+        dl = keep.tile([P, P], F32, align_bytes=64)
+        dr = keep.tile([P, 136], F32, align_bytes=64)
+        lt = keep.tile([P, P], F32)
+        rt1 = keep.tile([P, P], F32)
         ident_b = keep.tile([P, P], BF16, align_bytes=64)
         ident_f = keep.tile([P, P], F32, align_bytes=64)
-        ident_2 = keep.tile([P, 32, 2], BF16, align_bytes=64)
 
         def load_planes(planes, scales):
             for q in range(4):
@@ -74,42 +79,44 @@ def tile_dcblock_w_kernel(
                 in_=dram.rearrange("g p n t -> p g (n t)")[:, g0:g0 + gn, T * c0:T * (c0 + cn)].bitcast(I32),
             )
 
-        nc.gpsimd.memset(small[:].bitcast(I32), 0)
-        make_identity(nc, ident_b[:])
+        warm = keep.tile([P, 1], F32)
+        nc.vector.memset(warm[:], 1.0)
+        nc.vector.memset(wf_planes[:].bitcast(I32), 0)
+        nc.vector.memset(small[32:64, :].bitcast(I32), 0)
+        nc.vector.memset(small[64:P, :].bitcast(I32), 0)
+        nc.vector.memset(dr[:], 0.0)
+        nc.vector.memset(wu_planes[:].bitcast(I32), 0)
+        nc.vector.memset(dl[:], 1.0)
         for v, vec in enumerate((bn_var, bn_gamma, bn_mean, bn_beta)):
-            nc.sync.dma_start(out=small[4 * v:4 * v + 4, :], in_=vec.rearrange("(g k) -> g k", g=G))
-        nc.vector.memset(dl[:], -1.0)
-        nc.gpsimd.dma_start(out=dl[0:CP, :], in_=coarse_probs.rearrange("b c h w -> (b c) (h w)"))
+            nc.sync.dma_start(out=small[8 * v:8 * v + 8, :],
+                              in_=vec.rearrange("(g k) -> g k", g=G).unsqueeze(1).to_broadcast([G, 2, 512]))
         nc.sync.dma_start(
             out=x_sb[:].rearrange("p g t n -> p g (t n)"),
             in_=x.rearrange("b (g p t) h w -> p (b g) (t h w)", p=P, t=T),
         )
-        nc.vector.memset(dr[:, ZCOL:DCOLS], 0.0)
-        nc.scalar.dma_start(out=dr[32:33, SCOL:SCOL + 1], in_=sigma.unsqueeze(0))
-        warm = keep.tile([P, 1], F32)
-        nc.vector.memset(warm[:], 1.0)
-        nc.scalar.activation(out=warm[:], in_=warm[:], func=ACT.Sqrt)
-        nc.vector.tensor_copy(out=ident_2[:], in_=ident_b[:, 0:32].unsqueeze(2).to_broadcast([P, 32, 2]))
-        nc.vector.tensor_copy(
-            out=dr[:, 0:CP * P].bitcast(F32).rearrange("p (c n) -> p c n", c=CP),
-            in_=ident_2[:].rearrange("p c i -> p (c i)").bitcast(F32)[:, 0:CP].unsqueeze(2).to_broadcast([P, CP, P // 2]),
-        )
-        nc.sync.dma_start(out=dr[32:33, 0:CP * P], in_=coarse_probs.rearrange("b c h w -> b (c h w)"))
         load_words(wf_words, w_feat_words, 0, 1, 0, HALF)
-        nc.vector.tensor_copy(out=dr[0:32, ZCOL:ZCOL + CP], in_=ident_b[0:32, 0:CP])
-        nc.vector.memset(wf_planes[:].bitcast(I32), 0)
+        for r0, c0, c1 in ((0, 0, 16), (64, 15, CP)):
+            nc.scalar.dma_start(
+                out=p4[r0:r0 + ROWS * (c1 - c0), :],
+                in_=coarse_probs.rearrange("b c h w -> (b c) (h w)")[c0:c1].unsqueeze(1).to_broadcast([c1 - c0, ROWS, P]),
+            )
+        nc.scalar.activation(out=warm[:], in_=warm[:], func=ACT.Sqrt)
+        nc.scalar.dma_start(out=p4[SIGR:SIGR + 1, 0:1], in_=sigma.unsqueeze(0))
         load_planes(wf_planes, w_feat_scales)
         load_words(wf_words, w_feat_words, 1, 1, 0, HALF)
         load_words(wf_words, w_feat_words, 2, 2, 0, HALF)
         load_words(wf_words, w_feat_words, 0, 2, HALF, HALF)
-        load_words(wf_words, w_feat_words, 2, 2, HALF, HALF)
-        nc.vector.tensor_copy(out=ident_f[:], in_=ident_b[:])
-        nc.vector.memset(wu_planes[:].bitcast(I32), 0)
+        load_words(wf_words, w_feat_words, 2, 1, HALF, HALF)
+        load_words(wf_words, w_feat_words, 3, 1, HALF, HALF)
         load_planes(wu_planes, w_fuse_scales)
         for piece in ((0, 2, 0, HALF), (2, 2, 0, HALF), (0, 2, HALF, HALF), (2, 1, HALF, HALF),
                       (3, 1, HALF, NCH), (3, 1, HALF + NCH, NCH)):
             load_words(wu_words, w_fuse_words, *piece)
 
+        make_identity(nc, ident_b[:])
+        sel = keep.tile([P, ROWS, CP + 1], F32)
+        nc.gpsimd.iota(sel[:], pattern=[[1, ROWS], [ROWS, CP + 1]], base=0, channel_multiplier=-1,
+                       allow_small_or_imprecise_dtypes=True)
         pidx = keep.tile([P, 1], I32)
         nc.gpsimd.iota(pidx[:], pattern=[[0, 1]], base=0, channel_multiplier=1)
         wcol = keep.tile([P, 8, 16], F32)
@@ -118,65 +125,60 @@ def tile_dcblock_w_kernel(
         dlin = keep.tile([P, P], F32)
         nc.gpsimd.iota(dlin[:], pattern=[[1, P]], base=0, channel_multiplier=-1,
                        allow_small_or_imprecise_dtypes=True)
-        wrow_i = keep.tile([P, 1], I32)
-        nc.vector.tensor_single_scalar(out=wrow_i[:], in_=pidx[:], scalar=15, op=ALU.bitwise_and)
-        wrow = keep.tile([P, 1], F32)
-        nc.vector.tensor_copy(out=wrow[:], in_=wrow_i[:])
-        dw = keep.tile([P, P], F32)
-        mask = keep.tile([P, P], F32)
-        nc.gpsimd.tensor_tensor(out=dlin[:], in0=dlin[:], in1=dlin[:], op=ALU.mult)
-        nc.gpsimd.tensor_scalar(out=dlin[:], in0=dlin[:], scalar1=2652.25, scalar2=None, op0=ALU.is_le)
-        nc.gpsimd.tensor_scalar(out=dw[:], in0=wcol[:].rearrange("p h w -> p (h w)"), scalar1=wrow[:, 0:1],
-                                scalar2=None, op0=ALU.subtract)
-        nc.gpsimd.tensor_tensor(out=dw[:], in0=dw[:], in1=dw[:], op=ALU.mult)
-        nc.gpsimd.tensor_scalar(out=dw[:], in0=dw[:], scalar1=9.5, scalar2=None, op0=ALU.is_le)
-        nc.gpsimd.tensor_tensor(out=mask[:], in0=dw[:], in1=dlin[:], op=ALU.mult)
 
         ps_bn = bank(6, [P, T, P], BF16, "ps_bn")
         for t in range(T):
             nc.tensor.transpose(ps_bn[:, t, :], small[:, t:512:T], ident_b[:])
-        bn = keep.tile([P, 4, G * T], F32)
-        nc.vector.tensor_copy(
-            out=bn[:].rearrange("p v (g t) -> p (v g) t", t=T),
-            in_=ps_bn[:, :, 0:16].rearrange("p t r -> p r t"),
-        )
-        ve = keep.tile([P, G * T], F32)
+        hot = keep.tile([P, ROWS], F32)
+        m2 = keep.tile([P, 1], F32)
+        wrow_i = keep.tile([P, 1], I32)
+        wrow = keep.tile([P, 1], F32)
+        dw = keep.tile([P, P], F32)
+        mask = keep.tile([P, P], F32)
+        nc.vector.tensor_copy(out=ident_f[:], in_=ident_b[:])
+        ones = keep.tile([P, P], F32)
+        nc.vector.memset(ones[:], 1.0)
+        lop = slice(0, KD)
+        nc.vector.tensor_scalar(out=sel[:], in0=sel[:], scalar1=0.0, scalar2=None, op0=ALU.is_equal)
+        nc.vector.tensor_reduce(out=hot[:], in_=sel[:], axis=AX.X, op=ALU.add)
+        nc.vector.memset(hot[64:64 + ROWS, :], 0.0)
+        nc.vector.tensor_scalar(out=m2[:], in0=hot[:, 1:2], scalar1=-2.0, scalar2=None, op0=ALU.mult)
+        nc.vector.tensor_copy(out=dr[lop, OUTC:OUTC + 1], in_=hot[lop, 0:1])
+        nc.vector.tensor_single_scalar(out=wrow_i[:], in_=pidx[:], scalar=15, op=ALU.bitwise_and)
+        nc.vector.tensor_copy(out=wrow[:], in_=wrow_i[:])
+        nc.vector.tensor_tensor(out=dlin[:], in0=dlin[:], in1=dlin[:], op=ALU.mult)
+        nc.vector.tensor_scalar(out=dw[:], in0=wcol[:].rearrange("p h w -> p (h w)"), scalar1=wrow[:, 0:1],
+                                scalar2=None, op0=ALU.subtract)
         rs = keep.tile([P, G * T], F32)
+        bn = keep.tile([P, 4, G * T], F32)
+        mg = keep.tile([P, G * T], F32)
         nt = keep.tile([P, G * T], F32)
         sc = keep.tile([P, G * T], F32)
         bi = keep.tile([P, G * T], F32)
-        nc.vector.tensor_scalar(out=ve[:], in0=bn[:, 0, :], scalar1=BN_EPS, scalar2=None, op0=ALU.add)
-        nc.scalar.activation(out=rs[:], in_=ve[:], func=ACT.Sqrt)
-        nc.scalar.activation(out=warm[:], in_=warm[:], func=ACT.Exp)
+        nc.scalar.activation(out=rs[:].rearrange("p (g t) -> p g t", t=T),
+                             in_=ps_bn[:, :, 0:8:2].rearrange("p t r -> p r t"), func=ACT.Sqrt, bias=BN_EPS)
+        nc.vector.tensor_copy(
+            out=bn[:].rearrange("p v (g t) -> p (v g) t", t=T),
+            in_=ps_bn[:, :, 0:32:2].rearrange("p t r -> p r t"),
+        )
         nc.vector.reciprocal(out=rs[:], in_=rs[:])
+        nc.vector.tensor_tensor(out=mg[:], in0=bn[:, 1, :], in1=bn[:, 2, :], op=ALU.mult)
         nc.vector.tensor_tensor(out=sc[:], in0=rs[:], in1=bn[:, 1, :], op=ALU.mult)
-        nc.vector.tensor_tensor(out=nt[:], in0=sc[:], in1=bn[:, 2, :], op=ALU.mult)
+        nc.vector.tensor_tensor(out=nt[:], in0=rs[:], in1=mg[:], op=ALU.mult)
+        nc.vector.tensor_scalar(out=dlin[:], in0=dlin[:], scalar1=2652.25, scalar2=None, op0=ALU.is_le)
         nc.vector.tensor_tensor(out=bi[:], in0=bn[:, 3, :], in1=nt[:], op=ALU.subtract)
-
-        ps_d = [bank(j, [P, NCH], F32, "ps_d%d" % j) for j in range(5)]
-        for j in range(5):
-            c0, c1 = j * NCH, min((j + 1) * NCH, DCOLS)
-            nc.tensor.matmul(ps_d[j][:, 0:c1 - c0], lhsT=dl[:], rhs=dr[:, c0:c1], start=True, stop=True)
-        sq = keep.tile([P, CP * P], F32)
-        dist0 = keep.tile([P, 1], F32)
-        junk = keep.tile([P, CP], F32)
-        for j in range(5):
-            c0, c1 = j * NCH, min((j + 1) * NCH, CP * P)
-            nc.scalar.activation(out=sq[:, c0:c1], in_=ps_d[j][:, 0:c1 - c0], func=ACT.Square)
-        nc.scalar.activation(out=junk[:], in_=ps_d[4][:, ZCOL - 2048:ZCOL - 2048 + CP], func=ACT.Square,
-                             accum_out=dist0[:])
-        ps_dist = bank(5, [P, P], F32, "ps_dist")
-
-        def add_squares(cs):
-            for c in cs:
-                nc.tensor.matmul(ps_dist[:], lhsT=sq[:, c * P:(c + 1) * P], rhs=ident_f[:], is_transpose=True,
-                                 start=(c == 0), stop=(c == CP - 1))
 
         def bn_apply(g):
             for t in range(T):
                 k = g * T + t
                 nc.vector.tensor_scalar(out=xn[:, g, t, :], in0=x_sb[:, g, t, :], scalar1=sc[:, k:k + 1],
                                         scalar2=bi[:, k:k + 1], op0=ALU.mult, op1=ALU.add)
+
+        def bn_apply_scalar(g):
+            for t in range(T):
+                k = g * T + t
+                nc.scalar.activation(out=xn[:, g, t, :], in_=x_sb[:, g, t, :], func=ACT.Identity,
+                                     scale=sc[:, k:k + 1], bias=bi[:, k:k + 1])
 
         def regroup(g):
             nc.vector.tensor_copy(out=xg[:, g, :, :], in_=xn[:, g, :, :].rearrange("p t n -> p n t"))
@@ -187,24 +189,47 @@ def tile_dcblock_w_kernel(
                 in_=xg[:, g, :, :].rearrange("p n t -> p (n t)"),
             )
 
+        for g in (1, 2, 3):
+            bn_apply_scalar(g)
+        nc.scalar.activation(out=warm[:], in_=warm[:], func=ACT.Exp)
         bn_apply(0)
-        bn_apply(1)
+        nc.vector.tensor_tensor(out=sq[lop, :], in0=p4[lop, :], in1=p4[lop, :], op=ALU.mult)
         regroup(0)
-        bn_apply(2)
+        nc.vector.tensor_scalar(out=lt[lop, :], in0=p4[lop, :], scalar1=m2[lop, 0:1], scalar2=hot[lop, 2:3],
+                                op0=ALU.mult, op1=ALU.add)
         quantise_x(0)
+        nc.vector.tensor_scalar(out=rt1[lop, :], in0=p4[lop, :], scalar1=hot[lop, 1:2], scalar2=hot[lop, 0:1],
+                                op0=ALU.mult, op1=ALU.add)
+        nc.vector.scalar_tensor_tensor(out=dl[lop, :], in0=sq[lop, :], scalar=hot[lop, 0:1], in1=lt[lop, :],
+                                       op0=ALU.mult, op1=ALU.add)
         regroup(1)
-        bn_apply(3)
+        nc.vector.tensor_copy(out=dr[SIGR:SIGR + 1, SIGC:SIGC + 1], in_=p4[SIGR:SIGR + 1, 0:1])
+        nc.vector.scalar_tensor_tensor(out=dr[lop, 0:P], in0=sq[lop, :], scalar=hot[lop, 2:3], in1=rt1[lop, :],
+                                       op0=ALU.mult, op1=ALU.add)
         quantise_x(1)
+        nc.vector.tensor_tensor(out=dw[:], in0=dw[:], in1=dw[:], op=ALU.mult)
         regroup(2)
+        nc.vector.scalar_tensor_tensor(out=mask[:], in0=dw[:], scalar=9.5, in1=dlin[:], op0=ALU.is_le, op1=ALU.mult)
+
+        ps_d = bank(5, [P, 136], F32, "ps_d")
         den = keep.tile([P, 1], F32)
-        nc.vector.tensor_scalar(out=den[:], in0=ps_d[4][:, SCOL - 2048:SCOL - 2047], scalar1=-1.0, scalar2=0.0,
-                                op0=ALU.mult, op1=ALU.max)
-        nc.vector.tensor_tensor(out=den[:], in0=den[:], in1=den[:], op=ALU.mult)
-        regroup(3)
-        nc.vector.tensor_scalar(out=den[:], in0=den[:], scalar1=-2.0, scalar2=-1e-8, op0=ALU.mult, op1=ALU.add)
-        quantise_x(2)
-        nc.vector.reciprocal(out=den[:], in_=den[:])
-        quantise_x(3)
+        ex = keep.tile([P, 136], F32)
+
+        def distances():
+            nc.tensor.matmul(ps_d[:, 0:SIGC + 1], lhsT=dl[:], rhs=dr[:, 0:SIGC + 1], start=True, stop=True)
+
+        def affinity():
+            nc.vector.tensor_scalar(out=den[:], in0=ps_d[:, SIGC:SIGC + 1], scalar1=0.0, scalar2=None, op0=ALU.max)
+            quantise_x(2)
+            nc.vector.tensor_tensor(out=den[:], in0=den[:], in1=den[:], op=ALU.mult)
+            nc.vector.tensor_scalar(out=den[:], in0=den[:], scalar1=-2.0, scalar2=-1e-8, op0=ALU.mult, op1=ALU.add)
+            regroup(3)
+            nc.vector.reciprocal(out=den[:], in_=den[:])
+            nc.vector.tensor_scalar(out=ex[:, 0:129], in0=ps_d[:, 0:129], scalar1=0.0, scalar2=den[:, 0:1],
+                                    op0=ALU.max, op1=ALU.mult)
+            nc.scalar.activation(out=ex[:, 0:129], in_=ex[:, 0:129], func=ACT.Exp)
+            nc.scalar.activation(out=ex[:, 0:129], in_=ex[:, 0:129], func=ACT.Exp, bias=-1.0)
+            quantise_x(3)
 
         mt = keep.tile([P, G, T, P], F32)
         m_bank = (6, 7, 0, 1)
@@ -221,12 +246,19 @@ def tile_dcblock_w_kernel(
                     )
 
         def messages_out(c):
-            nc.scalar.copy(out=mt[:, c, :, :], in_=ps_m[c][:].rearrange("q (p t) -> q t p", t=T))
+            src = ps_m[c][:].rearrange("q (p t) -> q t p", t=T)
+            if c % 2:
+                nc.vector.tensor_copy(out=mt[:, c, :, :], in_=src)
+            else:
+                nc.scalar.copy(out=mt[:, c, :, :], in_=src)
 
         def aggregate(c):
             ps_a = bank(2 + c, [P, T, P], F32, "ps_a%d" % c)
             for t in range(T):
                 nc.tensor.matmul(ps_a[:, t, :], lhsT=mt[:, c, t, :], rhs=aff[:], start=True, stop=True)
+            return ps_a
+
+        def divide(c, ps_a):
             nc.vector.tensor_tensor(out=ag[:, c, :, :], in0=ps_a[:].rearrange("p t n -> p n t"),
                                     in1=rsum[:].unsqueeze(2).to_broadcast([P, P, T]), op=ALU.mult)
 
@@ -236,85 +268,101 @@ def tile_dcblock_w_kernel(
                 in_=ag[:, c, :, :].rearrange("p n t -> p (n t)"),
             )
 
-        add_squares(range(CP))
-        messages(range(G), (0, 1))
-        messages((0, 1), (2, 3))
+        messages((0,), (0, 1))
+        distances()
+        affinity()
+        messages((1, 2, 3), (0, 1))
 
-        ex = keep.tile([P, 136], F32)
-        nc.scalar.activation(out=ex[:, 128:129], in_=dist0[:], func=ACT.Exp, scale=den[:, 0:1])
-        nc.scalar.activation(out=ex[:, 0:128], in_=ps_dist[:], func=ACT.Exp, scale=den[:, 0:1])
-        nc.scalar.activation(out=ex[:, 0:129], in_=ex[:, 0:129], func=ACT.Exp, bias=-1.0)
         n_out = keep.tile([P, 1], F32)
-        nc.vector.tensor_reduce(out=n_out[:], in_=mask[:], axis=AX.X, op=ALU.add)
-        nc.vector.tensor_scalar(out=n_out[:], in0=n_out[:], scalar1=-1.0, scalar2=49.0, op0=ALU.mult, op1=ALU.add)
         aff = keep.tile([P, P], F32)
         own = keep.tile([P, 1], F32)
         aff_s = keep.tile([P, P], F32)
-        ones = keep.tile([P, P], F32)
         rsum = keep.tile([P, P], F32)
-        nc.vector.memset(ones[:], 1.0)
+        nc.vector.tensor_reduce(out=n_out[:], in_=mask[:], axis=AX.X, op=ALU.add)
+        nc.vector.tensor_scalar(out=n_out[:], in0=n_out[:], scalar1=-1.0, scalar2=49.0, op0=ALU.mult, op1=ALU.add)
         nc.vector.tensor_tensor(out=aff[:], in0=ex[:, 0:P], in1=mask[:], op=ALU.mult)
         nc.vector.tensor_tensor(out=own[:], in0=ex[:, 128:129], in1=n_out[:], op=ALU.mult)
         nc.vector.scalar_tensor_tensor(out=aff_s[:], in0=ident_f[:], scalar=own[:, 0:1], in1=aff[:],
                                        op0=ALU.mult, op1=ALU.add)
+        messages_out(0)
+        messages_out(1)
+        messages((0, 1), (2, 3))
+        ps_a0 = aggregate(0)
         ps_s = bank(5, [P, P], F32, "ps_s")
         nc.tensor.matmul(ps_s[:], lhsT=ones[:], rhs=aff_s[:], start=True, stop=True)
         nc.vector.reciprocal(out=rsum[:], in_=ps_s[:])
-        messages_out(0)
-        messages_out(1)
-        aggregate(0)
-        aggregate(1)
-        quantise_agg(0)
         messages((2, 3), (2, 3))
+        divide(0, ps_a0)
+        ps_a1 = aggregate(1)
         messages_out(2)
         messages_out(3)
+        quantise_agg(0)
+        ps_a2 = aggregate(2)
+        divide(1, ps_a1)
+        ps_a3 = aggregate(3)
         quantise_agg(1)
-        aggregate(2)
-        aggregate(3)
+        divide(2, ps_a2)
         quantise_agg(2)
+        divide(3, ps_a3)
         quantise_agg(3)
 
         rt = keep.tile([P, G, T, P], F32)
         o_sb = keep.tile([P, G, T, P], F32)
         out_v = out.rearrange("b (g p t) h w -> p (b g) (t h w)", p=P, t=T)
-        ps_r = [bank(m_bank[c], [P, NCH], F32, "ps_r%d" % c) for c in range(G)]
+        HP = P // 2
+        ps_r = [bank(6, [P, NCH], F32, "ps_r0"), bank(7, [P, NCH], F32, "ps_r1"), bank(0, [P, NCH], F32, "ps_r2"),
+                bank(1, [P, NCH // 2], F32, "ps_r3a"), bank(5, [P, NCH // 2], F32, "ps_r3b")]
+        r_cols = [slice(0, 512), slice(512, 1024), slice(1024, 1536), slice(1536, 1792), slice(1792, 2048)]
 
-        def refine(c, gs):
-            cols = slice(c * NCH, (c + 1) * NCH)
+        def refine(i, gs):
+            cols = r_cols[i]
             for g in gs:
                 nc.tensor.matmul_mx(
-                    out=ps_r[c][:], lhsT=aq_words[:, g, :].bitcast(FP8X4), lhsT_scale=aq_planes[:, g, :],
+                    out=ps_r[i][:], lhsT=aq_words[:, g, :].bitcast(FP8X4), lhsT_scale=aq_planes[:, g, :],
                     rhs=wu_words[:, g, cols].bitcast(FP8X4), rhs_scale=wu_planes[4 * g:P, cols],
                     start=(g == 0), stop=(g == G - 1),
                 )
 
-        def refined_out(c):
-            src = ps_r[c][:].rearrange("q (p t) -> q t p", t=T)
-            nc.scalar.copy(out=rt[:, c, 0:2, :], in_=src[:, 0:2, :])
-            nc.vector.tensor_copy(out=rt[:, c, 2:4, :], in_=src[:, 2:4, :])
+        def refined_out(i, engine_copy, c, p0, p1):
+            engine_copy(out=rt[:, c, :, p0:p1], in_=ps_r[i][:].rearrange("q (p t) -> q t p", t=T))
 
-        def finish(c, eng):
+        def finish(c):
             ps_o = bank(2 + c, [P, T, P], F32, "ps_o%d" % c)
             for t in range(T):
                 nc.tensor.transpose(ps_o[:, t, :], rt[:, c, t, :], ident_f[:])
             nc.vector.tensor_tensor(out=o_sb[:, c, :, :], in0=ps_o[:], in1=x_sb[:, c, :, :], op=ALU.add)
-            eng.dma_start(out=out_v[:, c, :], in_=o_sb[:, c, :, :].rearrange("p t n -> p (t n)"))
+            nc.sync.dma_start(out=out_v[:, c, :], in_=o_sb[:, c, :, :].rearrange("p t n -> p (t n)"))
 
         refine(0, (0, 1))
         refine(1, (0, 1))
         refine(0, (2, 3))
-        refined_out(0)
+        refined_out(0, nc.scalar.copy, 0, 0, P)
         refine(1, (2, 3))
-        refined_out(1)
-        finish(0, nc.scalar)
-        refine(2, (0,))
-        refine(3, (0,))
-        finish(1, nc.scalar)
-        refine(2, (1, 2))
-        refine(3, (1, 2))
+        refined_out(1, nc.vector.tensor_copy, 1, 0, P)
+        refine(2, (0, 1))
+        refine(3, (0, 1))
+        refine(4, (0, 1))
+        finish(0)
+        finish(1)
+        refine(2, (2,))
+        refine(3, (2,))
+        refine(4, (2,))
+        ps_oa = bank(6, [P, 2, P], F32, "ps_oa")
+        ps_ob = bank(7, [P, 2, P], F32, "ps_ob")
+        nc.tensor.matmul(ps_ob[:], lhsT=ident_b[:], rhs=x_sb[:, 3, 2:4, :], start=True, stop=False)
         refine(2, (3,))
-        refined_out(2)
+        refined_out(2, nc.scalar.copy, 2, 0, P)
         refine(3, (3,))
-        refined_out(3)
-        finish(2, nc.sync)
-        finish(3, nc.sync)
+        refine(4, (3,))
+        refined_out(3, nc.scalar.copy, 3, 0, HP)
+        refined_out(4, nc.vector.tensor_copy, 3, HP, P)
+        finish(2)
+        for t in (0, 1):
+            nc.tensor.transpose(ps_oa[:, t, :], rt[:, 3, t, :], ident_f[:])
+        for t in (2, 3):
+            nc.tensor.matmul(ps_ob[:, t - 2, :], lhsT=rt[:, 3, t, :], rhs=ident_f[:], is_transpose=True,
+                             start=False, stop=(t == 3))
+        nc.vector.tensor_tensor(out=o_sb[:, 3, 0:2, :], in0=ps_oa[:], in1=x_sb[:, 3, 0:2, :], op=ALU.add)
+        nc.scalar.copy(out=o_sb[:, 3, 2:4, :], in_=ps_ob[:])
+        for t0, eng in ((0, nc.sync), (2, nc.scalar)):
+            eng.dma_start(out=out_v[:, 3, t0 * P:(t0 + 2) * P], in_=o_sb[:, 3, t0:t0 + 2, :].rearrange("p t n -> p (t n)"))

@@ -65,6 +65,8 @@ def tile_dcblock_w_kernel(
         rt1 = keep.tile([P, P], F32)
         ident_b = keep.tile([P, P], BF16, align_bytes=64)
         ident_f = keep.tile([P, P], F32, align_bytes=64)
+        spread = keep.tile([P, 4 * P + 4], BF16, align_bytes=64)
+        x_nat = keep.tile([P, 4, P], F32)
 
         def load_planes(planes, scales):
             for q in range(4):
@@ -109,8 +111,8 @@ def tile_dcblock_w_kernel(
         load_words(wf_words, w_feat_words, 2, 1, HALF, HALF)
         load_words(wf_words, w_feat_words, 3, 1, HALF, HALF)
         load_planes(wu_planes, w_fuse_scales)
-        for piece in ((0, 2, 0, HALF), (2, 2, 0, HALF), (0, 2, HALF, HALF), (2, 1, HALF, HALF),
-                      (3, 1, HALF, NCH), (3, 1, HALF + NCH, NCH)):
+        for piece in ((0, 2, 0, HALF), (2, 2, 0, HALF), (0, 4, HALF, NCH),
+                      (0, 2, HALF + NCH, NCH), (2, 1, HALF + NCH, NCH), (3, 1, HALF + NCH, NCH)):
             load_words(wu_words, w_fuse_words, *piece)
 
         make_identity(nc, ident_b[:])
@@ -126,9 +128,17 @@ def tile_dcblock_w_kernel(
         nc.gpsimd.iota(dlin[:], pattern=[[1, P]], base=0, channel_multiplier=-1,
                        allow_small_or_imprecise_dtypes=True)
 
+        nc.gpsimd.memset(spread[:].bitcast(I32), 0)
+        nc.gpsimd.tensor_copy(out=spread[:, 3:3 + 4 * P:4], in_=ident_b[:])
+
         ps_bn = bank(6, [P, T, P], BF16, "ps_bn")
         for t in range(T):
             nc.tensor.transpose(ps_bn[:, t, :], small[:, t:512:T], ident_b[:])
+        ps_x = bank(4, [P, 4, P], F32, "ps_x")
+        for j in range(4):
+            for t in range(T):
+                nc.tensor.matmul(ps_x[:, j, :], lhsT=spread[:, P * j + 3 - t:P * j + 3 - t + P], rhs=x_sb[:, 3, t, :],
+                                 start=(t == 0), stop=(t == T - 1))
         hot = keep.tile([P, ROWS], F32)
         m2 = keep.tile([P, 1], F32)
         wrow_i = keep.tile([P, 1], I32)
@@ -272,6 +282,7 @@ def tile_dcblock_w_kernel(
         distances()
         affinity()
         messages((1, 2, 3), (0, 1))
+        nc.scalar.copy(out=x_nat[:], in_=ps_x[:])
 
         n_out = keep.tile([P, 1], F32)
         aff = keep.tile([P, P], F32)
@@ -309,22 +320,30 @@ def tile_dcblock_w_kernel(
         rt = keep.tile([P, G, T, P], F32)
         o_sb = keep.tile([P, G, T, P], F32)
         out_v = out.rearrange("b (g p t) h w -> p (b g) (t h w)", p=P, t=T)
-        HP = P // 2
-        ps_r = [bank(6, [P, NCH], F32, "ps_r0"), bank(7, [P, NCH], F32, "ps_r1"), bank(0, [P, NCH], F32, "ps_r2"),
-                bank(1, [P, NCH // 2], F32, "ps_r3a"), bank(5, [P, NCH // 2], F32, "ps_r3b")]
-        r_cols = [slice(0, 512), slice(512, 1024), slice(1024, 1536), slice(1536, 1792), slice(1792, 2048)]
+        out_d = out.rearrange("b (j p) h w -> p (b j) (h w)", p=P)
+        ps_r = [bank(i, [P, NCH], F32, "ps_r%d" % c) for c, i in enumerate((6, 7, 0))]
 
-        def refine(i, gs):
-            cols = r_cols[i]
+        def refine(c, gs):
+            cols = slice(c * NCH, (c + 1) * NCH)
             for g in gs:
                 nc.tensor.matmul_mx(
-                    out=ps_r[i][:], lhsT=aq_words[:, g, :].bitcast(FP8X4), lhsT_scale=aq_planes[:, g, :],
+                    out=ps_r[c][:], lhsT=aq_words[:, g, :].bitcast(FP8X4), lhsT_scale=aq_planes[:, g, :],
                     rhs=wu_words[:, g, cols].bitcast(FP8X4), rhs_scale=wu_planes[4 * g:P, cols],
                     start=(g == 0), stop=(g == G - 1),
                 )
 
-        def refined_out(i, engine_copy, c, p0, p1):
-            engine_copy(out=rt[:, c, :, p0:p1], in_=ps_r[i][:].rearrange("q (p t) -> q t p", t=T))
+        def refine_direct(gs):
+            for g in gs:
+                for j in range(4):
+                    cols = slice(3 * NCH + j * P, 3 * NCH + (j + 1) * P)
+                    nc.tensor.matmul_mx(
+                        out=ps_q[j][:], lhsT=wu_words[:, g, cols].bitcast(FP8X4), lhsT_scale=wu_planes[4 * g:P, cols],
+                        rhs=aq_words[:, g, :].bitcast(FP8X4), rhs_scale=aq_planes[:, g, :],
+                        start=(g == 0), stop=(g == G - 1),
+                    )
+
+        def refined_out(c, engine_copy):
+            engine_copy(out=rt[:, c, :, :], in_=ps_r[c][:].rearrange("q (p t) -> q t p", t=T))
 
         def finish(c):
             ps_o = bank(2 + c, [P, T, P], F32, "ps_o%d" % c)
@@ -336,33 +355,20 @@ def tile_dcblock_w_kernel(
         refine(0, (0, 1))
         refine(1, (0, 1))
         refine(0, (2, 3))
-        refined_out(0, nc.scalar.copy, 0, 0, P)
+        refined_out(0, nc.scalar.copy)
         refine(1, (2, 3))
-        refined_out(1, nc.vector.tensor_copy, 1, 0, P)
-        refine(2, (0, 1))
-        refine(3, (0, 1))
-        refine(4, (0, 1))
+        refined_out(1, nc.vector.tensor_copy)
+        refine(2, range(G))
+        refined_out(2, nc.scalar.copy)
         finish(0)
         finish(1)
-        refine(2, (2,))
-        refine(3, (2,))
-        refine(4, (2,))
-        ps_oa = bank(6, [P, 2, P], F32, "ps_oa")
-        ps_ob = bank(7, [P, 2, P], F32, "ps_ob")
-        nc.tensor.matmul(ps_ob[:], lhsT=ident_b[:], rhs=x_sb[:, 3, 2:4, :], start=True, stop=False)
-        refine(2, (3,))
-        refined_out(2, nc.scalar.copy, 2, 0, P)
-        refine(3, (3,))
-        refine(4, (3,))
-        refined_out(3, nc.scalar.copy, 3, 0, HP)
-        refined_out(4, nc.vector.tensor_copy, 3, HP, P)
+        ps_q = [bank(i, [P, P], F32, "ps_q%d" % j) for j, i in enumerate((1, 5, 6, 7))]
+        refine_direct((0, 1))
         finish(2)
-        for t in (0, 1):
-            nc.tensor.transpose(ps_oa[:, t, :], rt[:, 3, t, :], ident_f[:])
-        for t in (2, 3):
-            nc.tensor.matmul(ps_ob[:, t - 2, :], lhsT=rt[:, 3, t, :], rhs=ident_f[:], is_transpose=True,
-                             start=False, stop=(t == 3))
-        nc.vector.tensor_tensor(out=o_sb[:, 3, 0:2, :], in0=ps_oa[:], in1=x_sb[:, 3, 0:2, :], op=ALU.add)
-        nc.scalar.copy(out=o_sb[:, 3, 2:4, :], in_=ps_ob[:])
-        for t0, eng in ((0, nc.sync), (2, nc.scalar)):
-            eng.dma_start(out=out_v[:, 3, t0 * P:(t0 + 2) * P], in_=o_sb[:, 3, t0:t0 + 2, :].rearrange("p t n -> p (t n)"))
+        refine_direct((2,))
+        refine_direct((3,))
+        for j in range(4):
+            nc.vector.tensor_tensor(out=o_sb[:, 3, j, :], in0=ps_q[j][:], in1=x_nat[:, j, :], op=ALU.add)
+            if j % 2:
+                eng = nc.scalar if j == 1 else nc.sync
+                eng.dma_start(out=out_d[:, 11 + j:13 + j, :], in_=o_sb[:, 3, j - 1:j + 1, :])

@@ -96,17 +96,16 @@ def tile_dcblock_w_kernel(
             out=x_sb[:].rearrange("p g t n -> p g (t n)"),
             in_=x.rearrange("b (g p t) h w -> p (b g) (t h w)", p=P, t=T),
         )
-        load_words(wf_words, w_feat_words, 0, 1, 0, HALF)
         for r0, c0, c1 in ((0, 0, 16), (64, 15, CP)):
             nc.scalar.dma_start(
                 out=p4[r0:r0 + ROWS * (c1 - c0), :],
                 in_=coarse_probs.rearrange("b c h w -> (b c) (h w)")[c0:c1].unsqueeze(1).to_broadcast([c1 - c0, ROWS, P]),
             )
         nc.scalar.activation(out=warm[:], in_=warm[:], func=ACT.Sqrt)
-        nc.scalar.dma_start(out=p4[SIGR:SIGR + 1, 0:1], in_=sigma.unsqueeze(0))
+        load_words(wf_words, w_feat_words, 0, 2, 0, HALF)
         load_planes(wf_planes, w_feat_scales)
-        load_words(wf_words, w_feat_words, 1, 1, 0, HALF)
         load_words(wf_words, w_feat_words, 2, 2, 0, HALF)
+        nc.scalar.dma_start(out=p4[SIGR:SIGR + 1, 0:1], in_=sigma.unsqueeze(0))
         load_words(wf_words, w_feat_words, 0, 2, HALF, HALF)
         load_words(wf_words, w_feat_words, 2, 1, HALF, HALF)
         load_words(wf_words, w_feat_words, 3, 1, HALF, HALF)

@@ -110,8 +110,8 @@ def tile_dcblock_w_kernel(
         load_words(wf_words, w_feat_words, 2, 1, HALF, HALF)
         load_words(wf_words, w_feat_words, 3, 1, HALF, HALF)
         load_planes(wu_planes, w_fuse_scales)
-        for piece in ((0, 2, 0, HALF), (2, 2, 0, HALF), (0, 4, HALF, NCH),
-                      (0, 2, HALF + NCH, NCH), (2, 1, HALF + NCH, NCH), (3, 1, HALF + NCH, NCH)):
+        for piece in ((0, 2, 0, HALF), (2, 2, 0, HALF), (0, 2, HALF, HALF), (2, 2, HALF, NCH),
+                      (2, 1, HALF + NCH, NCH), (3, 1, HALF + NCH, NCH)):
             load_words(wu_words, w_fuse_words, *piece)
 
         make_identity(nc, ident_b[:])
@@ -320,13 +320,13 @@ def tile_dcblock_w_kernel(
         o_sb = keep.tile([P, G, T, P], F32)
         out_v = out.rearrange("b (g p t) h w -> p (b g) (t h w)", p=P, t=T)
         out_d = out.rearrange("b (j p) h w -> p (b j) (h w)", p=P)
-        ps_r = [bank(i, [P, NCH], F32, "ps_r%d" % c) for c, i in enumerate((6, 7, 0))]
+        HP = P // 2
 
-        def refine(c, gs):
-            cols = slice(c * NCH, (c + 1) * NCH)
+        def refine(tile, c0, gs):
+            cols = slice(c0, c0 + tile.shape[1])
             for g in gs:
                 nc.tensor.matmul_mx(
-                    out=ps_r[c][:], lhsT=aq_words[:, g, :].bitcast(FP8X4), lhsT_scale=aq_planes[:, g, :],
+                    out=tile[:], lhsT=aq_words[:, g, :].bitcast(FP8X4), lhsT_scale=aq_planes[:, g, :],
                     rhs=wu_words[:, g, cols].bitcast(FP8X4), rhs_scale=wu_planes[4 * g:P, cols],
                     start=(g == 0), stop=(g == G - 1),
                 )
@@ -341,33 +341,48 @@ def tile_dcblock_w_kernel(
                         start=(g == 0), stop=(g == G - 1),
                     )
 
-        def refined_out(c, engine_copy):
-            engine_copy(out=rt[:, c, :, :], in_=ps_r[c][:].rearrange("q (p t) -> q t p", t=T))
+        def refined_out(engine_copy, tile, c, p0, p1):
+            engine_copy(out=rt[:, c, :, p0:p1], in_=tile[:].rearrange("q (p t) -> q t p", t=T))
 
-        def finish(c):
-            ps_o = bank(2 + c, [P, T, P], F32, "ps_o%d" % c)
+        def store(c, eng):
+            eng.dma_start(out=out_v[:, c, :], in_=o_sb[:, c, :, :].rearrange("p t n -> p (t n)"))
+
+        def finish(c, ps_o):
             for t in range(T):
                 nc.tensor.transpose(ps_o[:, t, :], rt[:, c, t, :], ident_f[:])
             nc.vector.tensor_tensor(out=o_sb[:, c, :, :], in0=ps_o[:], in1=x_sb[:, c, :, :], op=ALU.add)
-            nc.sync.dma_start(out=out_v[:, c, :], in_=o_sb[:, c, :, :].rearrange("p t n -> p (t n)"))
+            store(c, nc.sync)
 
-        refine(0, (0, 1))
-        refine(1, (0, 1))
-        refine(0, (2, 3))
-        refined_out(0, nc.scalar.copy)
-        refine(1, (2, 3))
-        refined_out(1, nc.vector.tensor_copy)
-        refine(2, range(G))
-        refined_out(2, nc.scalar.copy)
-        finish(0)
-        finish(1)
-        ps_q = [bank(i, [P, P], F32, "ps_q%d" % j) for j, i in enumerate((1, 5, 6, 7))]
+        ps_r0 = bank(6, [P, NCH], F32, "ps_r0")
+        ps_r1 = bank(7, [P, NCH], F32, "ps_r1")
+        refine(ps_r0, 0, (0, 1))
+        refine(ps_r1, NCH, (0, 1))
+        refine(ps_r0, 0, (2, 3))
+        refined_out(nc.scalar.copy, ps_r0, 0, 0, P)
+        refine(ps_r1, NCH, (2, 3))
+        refined_out(nc.vector.tensor_copy, ps_r1, 1, 0, P)
+        finish(0, bank(6, [P, T, P], F32, "ps_o0"))
+        ps_r2a = bank(0, [P, NCH // 2], F32, "ps_r2a")
+        ps_r2b = bank(4, [P, NCH // 2], F32, "ps_r2b")
+        ps_q = [bank(i, [P, P], F32, "ps_q%d" % j) for j, i in enumerate((1, 2, 3, 5))]
+        refine(ps_r2a, HALF, (0, 1))
+        refine(ps_r2b, HALF + NCH // 2, (0, 1))
         refine_direct((0, 1))
-        finish(2)
+        finish(1, bank(7, [P, T, P], F32, "ps_o1"))
+        ps_o2 = bank(6, [P, T, P], F32, "ps_o2")
+        nc.tensor.matmul(ps_o2[:], lhsT=ident_b[:], rhs=x_sb[:, 2, :, :], start=True, stop=False)
+        refine(ps_r2a, HALF, (2, 3))
+        refined_out(nc.scalar.copy, ps_r2a, 2, 0, HP)
+        refine(ps_r2b, HALF + NCH // 2, (2, 3))
+        refined_out(nc.vector.tensor_copy, ps_r2b, 2, HP, P)
         refine_direct((2,))
         refine_direct((3,))
+        for t in range(T):
+            nc.tensor.matmul(ps_o2[:, t, :], lhsT=rt[:, 2, t, :], rhs=ident_f[:], is_transpose=True,
+                             start=False, stop=(t == T - 1))
+        nc.scalar.copy(out=o_sb[:, 2, :, :], in_=ps_o2[:])
+        store(2, nc.scalar)
         for j in range(4):
             nc.vector.tensor_tensor(out=o_sb[:, 3, j, :], in0=ps_q[j][:], in1=x_nat[:, j, :], op=ALU.add)
             if j % 2:
-                eng = nc.scalar if j == 1 else nc.sync
-                eng.dma_start(out=out_d[:, 11 + j:13 + j, :], in_=o_sb[:, 3, j - 1:j + 1, :])
+                nc.sync.dma_start(out=out_d[:, 11 + j:13 + j, :], in_=o_sb[:, 3, j - 1:j + 1, :])

@@ -66,7 +66,7 @@ def tile_dcblock_w_kernel(
         ident_b = keep.tile([P, P], BF16, align_bytes=64)
         ident_f = keep.tile([P, P], F32, align_bytes=64)
         spread = keep.tile([P, 4 * P + 4], BF16, align_bytes=64)
-        x_nat = keep.tile([P, 4, P], F32)
+        x_nat = keep.tile([P, 2, 4, P], F32)
 
         def load_planes(planes, scales):
             for q in range(4):
@@ -110,8 +110,8 @@ def tile_dcblock_w_kernel(
         load_words(wf_words, w_feat_words, 2, 1, HALF, HALF)
         load_words(wf_words, w_feat_words, 3, 1, HALF, HALF)
         load_planes(wu_planes, w_fuse_scales)
-        for piece in ((0, 2, 0, HALF), (2, 2, 0, HALF), (0, 2, HALF, HALF), (2, 2, HALF, NCH),
-                      (2, 1, HALF + NCH, NCH), (3, 1, HALF + NCH, NCH)):
+        for piece in ((0, 2, 0, HALF), (2, 2, 0, HALF), (0, 4, HALF, NCH),
+                      (0, 2, HALF + NCH, NCH), (2, 1, HALF + NCH, NCH), (3, 1, HALF + NCH, NCH)):
             load_words(wu_words, w_fuse_words, *piece)
 
         make_identity(nc, ident_b[:])
@@ -133,11 +133,12 @@ def tile_dcblock_w_kernel(
         ps_bn = bank(6, [P, T, P], BF16, "ps_bn")
         for t in range(T):
             nc.tensor.transpose(ps_bn[:, t, :], small[:, t:512:T], ident_b[:])
-        ps_x = bank(4, [P, 4, P], F32, "ps_x")
-        for j in range(4):
-            for t in range(T):
-                nc.tensor.matmul(ps_x[:, j, :], lhsT=spread[:, P * j + 3 - t:P * j + 3 - t + P], rhs=x_sb[:, 3, t, :],
-                                 start=(t == 0), stop=(t == T - 1))
+        ps_x = [bank(i, [P, 4, P], F32, "ps_x%d" % b) for b, i in enumerate((4, 3))]
+        for b in range(2):
+            for j in range(4):
+                for t in range(T):
+                    nc.tensor.matmul(ps_x[b][:, j, :], lhsT=spread[:, P * j + 3 - t:P * j + 3 - t + P],
+                                     rhs=x_sb[:, 2 + b, t, :], start=(t == 0), stop=(t == T - 1))
         hot = keep.tile([P, ROWS], F32)
         m2 = keep.tile([P, 1], F32)
         wrow_i = keep.tile([P, 1], I32)
@@ -281,7 +282,6 @@ def tile_dcblock_w_kernel(
         distances()
         affinity()
         messages((1, 2, 3), (0, 1))
-        nc.scalar.copy(out=x_nat[:], in_=ps_x[:])
 
         n_out = keep.tile([P, 1], F32)
         aff = keep.tile([P, P], F32)
@@ -296,6 +296,8 @@ def tile_dcblock_w_kernel(
                                        op0=ALU.mult, op1=ALU.add)
         messages_out(0)
         messages_out(1)
+        for b in range(2):
+            nc.scalar.copy(out=x_nat[:, b, :, :], in_=ps_x[b][:])
         messages((0, 1), (2, 3))
         ps_a0 = aggregate(0)
         ps_s = bank(5, [P, P], F32, "ps_s")
@@ -320,10 +322,8 @@ def tile_dcblock_w_kernel(
         o_sb = keep.tile([P, G, T, P], F32)
         out_v = out.rearrange("b (g p t) h w -> p (b g) (t h w)", p=P, t=T)
         out_d = out.rearrange("b (j p) h w -> p (b j) (h w)", p=P)
-        HP = P // 2
-
-        def refine(tile, c0, gs):
-            cols = slice(c0, c0 + tile.shape[1])
+        def refine(tile, c, gs):
+            cols = slice(c * NCH, (c + 1) * NCH)
             for g in gs:
                 nc.tensor.matmul_mx(
                     out=tile[:], lhsT=aq_words[:, g, :].bitcast(FP8X4), lhsT_scale=aq_planes[:, g, :],
@@ -331,58 +331,43 @@ def tile_dcblock_w_kernel(
                     start=(g == 0), stop=(g == G - 1),
                 )
 
-        def refine_direct(gs):
+        def refine_direct(tile, c, j, gs):
+            cols = slice(c * NCH + j * P, c * NCH + (j + 1) * P)
             for g in gs:
-                for j in range(4):
-                    cols = slice(3 * NCH + j * P, 3 * NCH + (j + 1) * P)
-                    nc.tensor.matmul_mx(
-                        out=ps_q[j][:], lhsT=wu_words[:, g, cols].bitcast(FP8X4), lhsT_scale=wu_planes[4 * g:P, cols],
-                        rhs=aq_words[:, g, :].bitcast(FP8X4), rhs_scale=aq_planes[:, g, :],
-                        start=(g == 0), stop=(g == G - 1),
-                    )
-
-        def refined_out(engine_copy, tile, c, p0, p1):
-            engine_copy(out=rt[:, c, :, p0:p1], in_=tile[:].rearrange("q (p t) -> q t p", t=T))
-
-        def store(c, eng):
-            eng.dma_start(out=out_v[:, c, :], in_=o_sb[:, c, :, :].rearrange("p t n -> p (t n)"))
+                nc.tensor.matmul_mx(
+                    out=tile[:], lhsT=wu_words[:, g, cols].bitcast(FP8X4), lhsT_scale=wu_planes[4 * g:P, cols],
+                    rhs=aq_words[:, g, :].bitcast(FP8X4), rhs_scale=aq_planes[:, g, :],
+                    start=(g == 0), stop=(g == G - 1),
+                )
 
         def finish(c, ps_o):
             for t in range(T):
                 nc.tensor.transpose(ps_o[:, t, :], rt[:, c, t, :], ident_f[:])
             nc.vector.tensor_tensor(out=o_sb[:, c, :, :], in0=ps_o[:], in1=x_sb[:, c, :, :], op=ALU.add)
-            store(c, nc.sync)
+            nc.sync.dma_start(out=out_v[:, c, :], in_=o_sb[:, c, :, :].rearrange("p t n -> p (t n)"))
 
-        ps_r0 = bank(6, [P, NCH], F32, "ps_r0")
-        ps_r1 = bank(7, [P, NCH], F32, "ps_r1")
-        refine(ps_r0, 0, (0, 1))
-        refine(ps_r1, NCH, (0, 1))
-        refine(ps_r0, 0, (2, 3))
-        refined_out(nc.scalar.copy, ps_r0, 0, 0, P)
-        refine(ps_r1, NCH, (2, 3))
-        refined_out(nc.vector.tensor_copy, ps_r1, 1, 0, P)
+        def add_direct(tile, c, j):
+            nc.vector.tensor_tensor(out=o_sb[:, c, j, :], in0=tile[:], in1=x_nat[:, c - 2, j, :], op=ALU.add)
+
+        ps_r = [bank(6, [P, NCH], F32, "ps_r0"), bank(7, [P, NCH], F32, "ps_r1")]
+        refine(ps_r[0], 0, (0, 1))
+        refine(ps_r[1], 1, (0, 1))
+        refine(ps_r[0], 0, (2, 3))
+        nc.scalar.copy(out=rt[:, 0, :, :], in_=ps_r[0][:].rearrange("q (p t) -> q t p", t=T))
+        refine(ps_r[1], 1, (2, 3))
+        nc.vector.tensor_copy(out=rt[:, 1, :, :], in_=ps_r[1][:].rearrange("q (p t) -> q t p", t=T))
         finish(0, bank(6, [P, T, P], F32, "ps_o0"))
-        ps_r2a = bank(0, [P, NCH // 2], F32, "ps_r2a")
-        ps_r2b = bank(4, [P, NCH // 2], F32, "ps_r2b")
-        ps_q = [bank(i, [P, P], F32, "ps_q%d" % j) for j, i in enumerate((1, 2, 3, 5))]
-        refine(ps_r2a, HALF, (0, 1))
-        refine(ps_r2b, HALF + NCH // 2, (0, 1))
-        refine_direct((0, 1))
         finish(1, bank(7, [P, T, P], F32, "ps_o1"))
-        ps_o2 = bank(6, [P, T, P], F32, "ps_o2")
-        nc.tensor.matmul(ps_o2[:], lhsT=ident_b[:], rhs=x_sb[:, 2, :, :], start=True, stop=False)
-        refine(ps_r2a, HALF, (2, 3))
-        refined_out(nc.scalar.copy, ps_r2a, 2, 0, HP)
-        refine(ps_r2b, HALF + NCH // 2, (2, 3))
-        refined_out(nc.vector.tensor_copy, ps_r2b, 2, HP, P)
-        refine_direct((2,))
-        refine_direct((3,))
-        for t in range(T):
-            nc.tensor.matmul(ps_o2[:, t, :], lhsT=rt[:, 2, t, :], rhs=ident_f[:], is_transpose=True,
-                             start=False, stop=(t == T - 1))
-        nc.scalar.copy(out=o_sb[:, 2, :, :], in_=ps_o2[:])
-        store(2, nc.scalar)
+        ps_q2 = [bank(i, [P, P], F32, "ps_q2%d" % j) for j, i in enumerate((0, 4, 1, 2))]
         for j in range(4):
-            nc.vector.tensor_tensor(out=o_sb[:, 3, j, :], in0=ps_q[j][:], in1=x_nat[:, j, :], op=ALU.add)
+            refine_direct(ps_q2[j], 2, j, range(G))
+            add_direct(ps_q2[j], 2, j)
+        nc.scalar.dma_start(out=out_d[:, 8:12, :], in_=o_sb[:, 2, :, :])
+        ps_q3 = [bank(i, [P, P], F32, "ps_q3%d" % j) for j, i in enumerate((3, 5, 6, 7))]
+        for gs in ((0, 1), (2,), (3,)):
+            for j in range(4):
+                refine_direct(ps_q3[j], 3, j, gs)
+        for j in range(4):
+            add_direct(ps_q3[j], 3, j)
             if j % 2:
                 nc.sync.dma_start(out=out_d[:, 11 + j:13 + j, :], in_=o_sb[:, 3, j - 1:j + 1, :])

@@ -65,8 +65,8 @@ def tile_dcblock_w_kernel(
         rt1 = keep.tile([P, P], F32)
         ident_b = keep.tile([P, P], BF16, align_bytes=64)
         ident_f = keep.tile([P, P], F32, align_bytes=64)
-        spread = keep.tile([P, 4 * P + 4], BF16, align_bytes=64)
-        x_nat = keep.tile([P, 2, 4, P], F32)
+        x_t = keep.tile([P, G, P, T], BF16)
+        x_nat = keep.tile([P, G, 4, P], BF16)
 
         def load_planes(planes, scales):
             for q in range(4):
@@ -102,16 +102,14 @@ def tile_dcblock_w_kernel(
                 in_=coarse_probs.rearrange("b c h w -> (b c) (h w)")[c0:c1].unsqueeze(1).to_broadcast([c1 - c0, ROWS, P]),
             )
         nc.scalar.activation(out=warm[:], in_=warm[:], func=ACT.Sqrt)
-        load_words(wf_words, w_feat_words, 0, 2, 0, HALF)
+        load_words(wf_words, w_feat_words, 0, 1, 0, C)
         load_planes(wf_planes, w_feat_scales)
-        load_words(wf_words, w_feat_words, 2, 2, 0, HALF)
+        load_words(wf_words, w_feat_words, 1, 1, 0, C)
         nc.scalar.dma_start(out=p4[SIGR:SIGR + 1, 0:1], in_=sigma.unsqueeze(0))
-        load_words(wf_words, w_feat_words, 0, 2, HALF, HALF)
-        load_words(wf_words, w_feat_words, 2, 1, HALF, HALF)
-        load_words(wf_words, w_feat_words, 3, 1, HALF, HALF)
+        load_words(wf_words, w_feat_words, 2, 1, 0, C)
+        load_words(wf_words, w_feat_words, 3, 1, 0, C)
         load_planes(wu_planes, w_fuse_scales)
-        for piece in ((0, 2, 0, HALF), (2, 2, 0, HALF), (0, 4, HALF, NCH),
-                      (0, 2, HALF + NCH, NCH), (2, 1, HALF + NCH, NCH), (3, 1, HALF + NCH, NCH)):
+        for piece in ((0, 4, 0, HALF), (0, 2, HALF, HALF), (2, 2, HALF, NCH), (2, 2, HALF + NCH, NCH)):
             load_words(wu_words, w_fuse_words, *piece)
 
         make_identity(nc, ident_b[:])
@@ -127,18 +125,32 @@ def tile_dcblock_w_kernel(
         nc.gpsimd.iota(dlin[:], pattern=[[1, P]], base=0, channel_multiplier=-1,
                        allow_small_or_imprecise_dtypes=True)
 
-        nc.gpsimd.memset(spread[:].bitcast(I32), 0)
-        nc.gpsimd.tensor_copy(out=spread[:, 3:3 + 4 * P:4], in_=ident_b[:])
-
         ps_bn = bank(6, [P, T, P], BF16, "ps_bn")
         for t in range(T):
             nc.tensor.transpose(ps_bn[:, t, :], small[:, t:512:T], ident_b[:])
-        ps_x = [bank(i, [P, 4, P], F32, "ps_x%d" % b) for b, i in enumerate((4, 3))]
-        for b in range(2):
-            for j in range(4):
+        def x_turn(pair, i):
+            ps_t = bank(i, [P, 2, T, P], BF16, "ps_t%d" % pair)
+            for b in range(2):
                 for t in range(T):
-                    nc.tensor.matmul(ps_x[b][:, j, :], lhsT=spread[:, P * j + 3 - t:P * j + 3 - t + P],
-                                     rhs=x_sb[:, 2 + b, t, :], start=(t == 0), stop=(t == T - 1))
+                    nc.tensor.transpose(ps_t[:, b, t, :], x_sb[:, 2 * pair + b, t, :], ident_b[:])
+            return ps_t
+
+        def x_turn_out(pair, ps_t):
+            for b in range(2):
+                nc.vector.tensor_copy(out=x_t[:, 2 * pair + b, :, :], in_=ps_t[:, b, :, :].rearrange("n t p -> n p t"))
+
+        def x_back(pair, i):
+            ps_x = bank(i, [P, 2, 4, P], BF16, "ps_x%d" % pair)
+            for b in range(2):
+                for j in range(4):
+                    nc.tensor.transpose(ps_x[:, b, j, :], x_t[:, 2 * pair + b, 32 * j:32 * (j + 1), :].rearrange("n p t -> n (p t)"), ident_b[:])
+            return ps_x
+
+        def x_back_out(pair, ps_x):
+            for b in range(2):
+                nc.scalar.copy(out=x_nat[:, 2 * pair + b, :, :], in_=ps_x[:, b, :, :])
+
+        ps_t = [x_turn(0, 4), x_turn(1, 3)]
         hot = keep.tile([P, ROWS], F32)
         m2 = keep.tile([P, 1], F32)
         wrow_i = keep.tile([P, 1], I32)
@@ -148,6 +160,9 @@ def tile_dcblock_w_kernel(
         nc.vector.tensor_copy(out=ident_f[:], in_=ident_b[:])
         ones = keep.tile([P, P], F32)
         nc.vector.memset(ones[:], 1.0)
+        other = keep.tile([P, 136], F32)
+        nc.vector.memset(other[:], 1.0)
+        nc.vector.tensor_scalar(out=other[:, 0:P], in0=ident_f[:], scalar1=-1.0, scalar2=1.0, op0=ALU.mult, op1=ALU.add)
         lop = slice(0, KD)
         nc.vector.tensor_scalar(out=sel[:], in0=sel[:], scalar1=0.0, scalar2=None, op0=ALU.is_equal)
         nc.vector.tensor_reduce(out=hot[:], in_=sel[:], axis=AX.X, op=ALU.add)
@@ -213,12 +228,14 @@ def tile_dcblock_w_kernel(
         nc.vector.scalar_tensor_tensor(out=dl[lop, :], in0=sq[lop, :], scalar=hot[lop, 0:1], in1=lt[lop, :],
                                        op0=ALU.mult, op1=ALU.add)
         regroup(1)
+        x_turn_out(0, ps_t[0])
         nc.vector.tensor_copy(out=dr[SIGR:SIGR + 1, SIGC:SIGC + 1], in_=p4[SIGR:SIGR + 1, 0:1])
         nc.vector.scalar_tensor_tensor(out=dr[lop, 0:P], in0=sq[lop, :], scalar=hot[lop, 2:3], in1=rt1[lop, :],
                                        op0=ALU.mult, op1=ALU.add)
         quantise_x(1)
         nc.vector.tensor_tensor(out=dw[:], in0=dw[:], in1=dw[:], op=ALU.mult)
         regroup(2)
+        x_turn_out(1, ps_t[1])
         nc.vector.scalar_tensor_tensor(out=mask[:], in0=dw[:], scalar=9.5, in1=dlin[:], op0=ALU.is_le, op1=ALU.mult)
 
         ps_d = bank(5, [P, 136], F32, "ps_d")
@@ -235,9 +252,9 @@ def tile_dcblock_w_kernel(
             nc.vector.tensor_scalar(out=den[:], in0=den[:], scalar1=-2.0, scalar2=-1e-8, op0=ALU.mult, op1=ALU.add)
             regroup(3)
             nc.vector.reciprocal(out=den[:], in_=den[:])
-            nc.vector.tensor_scalar(out=ex[:, 0:129], in0=ps_d[:, 0:129], scalar1=0.0, scalar2=den[:, 0:1],
-                                    op0=ALU.max, op1=ALU.mult)
-            nc.scalar.activation(out=ex[:, 0:129], in_=ex[:, 0:129], func=ACT.Exp)
+            nc.vector.scalar_tensor_tensor(out=ex[:, 0:129], in0=ps_d[:, 0:129], scalar=0.0, in1=other[:, 0:129],
+                                           op0=ALU.max, op1=ALU.mult)
+            nc.scalar.activation(out=ex[:, 0:129], in_=ex[:, 0:129], func=ACT.Exp, scale=den[:, 0:1])
             nc.scalar.activation(out=ex[:, 0:129], in_=ex[:, 0:129], func=ACT.Exp, bias=-1.0)
             quantise_x(3)
 
@@ -260,7 +277,8 @@ def tile_dcblock_w_kernel(
             if c % 2:
                 nc.vector.tensor_copy(out=mt[:, c, :, :], in_=src)
             else:
-                nc.scalar.copy(out=mt[:, c, :, :], in_=src)
+                for t in (0, 2):
+                    nc.scalar.copy(out=mt[:, c, t:t + 2, :], in_=src[:, t:t + 2, :])
 
         def aggregate(c):
             ps_a = bank(2 + c, [P, T, P], F32, "ps_a%d" % c)
@@ -278,10 +296,13 @@ def tile_dcblock_w_kernel(
                 in_=ag[:, c, :, :].rearrange("p n t -> p (n t)"),
             )
 
-        messages((0,), (0, 1))
+        messages((0,), range(G))
         distances()
         affinity()
-        messages((1, 2, 3), (0, 1))
+        ps_x = [x_back(0, 2), x_back(1, 4)]
+        messages((1, 2), range(G))
+        for pair in range(2):
+            x_back_out(pair, ps_x[pair])
 
         n_out = keep.tile([P, 1], F32)
         aff = keep.tile([P, P], F32)
@@ -294,22 +315,17 @@ def tile_dcblock_w_kernel(
         nc.vector.tensor_tensor(out=own[:], in0=ex[:, 128:129], in1=n_out[:], op=ALU.mult)
         nc.vector.scalar_tensor_tensor(out=aff_s[:], in0=ident_f[:], scalar=own[:, 0:1], in1=aff[:],
                                        op0=ALU.mult, op1=ALU.add)
-        messages_out(0)
-        messages_out(1)
-        for b in range(2):
-            nc.scalar.copy(out=x_nat[:, b, :, :], in_=ps_x[b][:])
-        messages((0, 1), (2, 3))
-        ps_a0 = aggregate(0)
         ps_s = bank(5, [P, P], F32, "ps_s")
         nc.tensor.matmul(ps_s[:], lhsT=ones[:], rhs=aff_s[:], start=True, stop=True)
+        messages((3,), range(G))
         nc.vector.reciprocal(out=rsum[:], in_=ps_s[:])
-        messages((2, 3), (2, 3))
-        divide(0, ps_a0)
+        for c in range(G):
+            messages_out(c)
+        ps_a0 = aggregate(0)
         ps_a1 = aggregate(1)
-        messages_out(2)
-        messages_out(3)
-        quantise_agg(0)
+        divide(0, ps_a0)
         ps_a2 = aggregate(2)
+        quantise_agg(0)
         divide(1, ps_a1)
         ps_a3 = aggregate(3)
         quantise_agg(1)
@@ -318,20 +334,10 @@ def tile_dcblock_w_kernel(
         divide(3, ps_a3)
         quantise_agg(3)
 
-        rt = keep.tile([P, G, T, P], F32)
-        o_sb = keep.tile([P, G, T, P], F32)
-        out_v = out.rearrange("b (g p t) h w -> p (b g) (t h w)", p=P, t=T)
-        out_d = out.rearrange("b (j p) h w -> p (b j) (h w)", p=P)
-        def refine(tile, c, gs):
-            cols = slice(c * NCH, (c + 1) * NCH)
-            for g in gs:
-                nc.tensor.matmul_mx(
-                    out=tile[:], lhsT=aq_words[:, g, :].bitcast(FP8X4), lhsT_scale=aq_planes[:, g, :],
-                    rhs=wu_words[:, g, cols].bitcast(FP8X4), rhs_scale=wu_planes[4 * g:P, cols],
-                    start=(g == 0), stop=(g == G - 1),
-                )
+        o_sb = keep.tile([P, G, 4, P], F32)
+        out_d = out.rearrange("b (c j p) h w -> p (b c) j (h w)", p=P, j=4)
 
-        def refine_direct(tile, c, j, gs):
+        def refine(tile, c, j, gs):
             cols = slice(c * NCH + j * P, c * NCH + (j + 1) * P)
             for g in gs:
                 nc.tensor.matmul_mx(
@@ -340,34 +346,31 @@ def tile_dcblock_w_kernel(
                     start=(g == 0), stop=(g == G - 1),
                 )
 
-        def finish(c, ps_o):
-            for t in range(T):
-                nc.tensor.transpose(ps_o[:, t, :], rt[:, c, t, :], ident_f[:])
-            nc.vector.tensor_tensor(out=o_sb[:, c, :, :], in0=ps_o[:], in1=x_sb[:, c, :, :], op=ALU.add)
-            nc.sync.dma_start(out=out_v[:, c, :], in_=o_sb[:, c, :, :].rearrange("p t n -> p (t n)"))
+        def add_x(tile, c, j):
+            nc.vector.tensor_tensor(out=o_sb[:, c, j, :], in0=tile[:], in1=x_nat[:, c, j, :], op=ALU.add)
 
-        def add_direct(tile, c, j):
-            nc.vector.tensor_tensor(out=o_sb[:, c, j, :], in0=tile[:], in1=x_nat[:, c - 2, j, :], op=ALU.add)
+        def store(c, j0, j1):
+            nc.sync.dma_start(out=out_d[:, c, j0:j1, :], in_=o_sb[:, c, j0:j1, :])
 
-        ps_r = [bank(6, [P, NCH], F32, "ps_r0"), bank(7, [P, NCH], F32, "ps_r1")]
-        refine(ps_r[0], 0, (0, 1))
-        refine(ps_r[1], 1, (0, 1))
-        refine(ps_r[0], 0, (2, 3))
-        nc.scalar.copy(out=rt[:, 0, :, :], in_=ps_r[0][:].rearrange("q (p t) -> q t p", t=T))
-        refine(ps_r[1], 1, (2, 3))
-        nc.vector.tensor_copy(out=rt[:, 1, :, :], in_=ps_r[1][:].rearrange("q (p t) -> q t p", t=T))
-        finish(0, bank(6, [P, T, P], F32, "ps_o0"))
-        finish(1, bank(7, [P, T, P], F32, "ps_o1"))
-        ps_q2 = [bank(i, [P, P], F32, "ps_q2%d" % j) for j, i in enumerate((0, 4, 1, 2))]
-        for j in range(4):
-            refine_direct(ps_q2[j], 2, j, range(G))
-            add_direct(ps_q2[j], 2, j)
-        nc.scalar.dma_start(out=out_d[:, 8:12, :], in_=o_sb[:, 2, :, :])
-        ps_q3 = [bank(i, [P, P], F32, "ps_q3%d" % j) for j, i in enumerate((3, 5, 6, 7))]
-        for gs in ((0, 1), (2,), (3,)):
+        def tiles(c, banks):
+            return [bank(i, [P, P], F32, "ps_r%d%d" % (c, j)) for j, i in enumerate(banks)]
+
+        ps_r = [tiles(0, (6, 7, 0, 1)), tiles(1, (2, 3, 4, 5))]
+        for gs in ((0, 1, 2), (3,)):
+            for c in range(2):
+                for j in range(4):
+                    refine(ps_r[c][j], c, j, gs)
+        for c in range(2):
             for j in range(4):
-                refine_direct(ps_q3[j], 3, j, gs)
-        for j in range(4):
-            add_direct(ps_q3[j], 3, j)
-            if j % 2:
-                nc.sync.dma_start(out=out_d[:, 11 + j:13 + j, :], in_=o_sb[:, 3, j - 1:j + 1, :])
+                add_x(ps_r[c][j], c, j)
+            store(c, 0, 4)
+        ps_r = {2: tiles(2, (6, 7, 0, 1)), 3: tiles(3, (2, 3, 4, 5))}
+        for c in (2, 3):
+            for gs in ((0, 1), (2, 3)):
+                for j in range(4):
+                    refine(ps_r[c][j], c, j, gs)
+            for j in range(4):
+                add_x(ps_r[c][j], c, j)
+                if c == 3 and j == 1:
+                    store(3, 0, 2)
+            store(c, 2 * (c - 2), 4)

@@ -137,7 +137,7 @@ def tile_dcblock_w_kernel(
 
         def x_turn_out(pair, ps_t):
             for b in range(2):
-                nc.vector.tensor_copy(out=x_t[:, 2 * pair + b, :, :], in_=ps_t[:, b, :, :].rearrange("n t p -> n p t"))
+                nc.scalar.copy(out=x_t[:, 2 * pair + b, :, :], in_=ps_t[:, b, :, :].rearrange("n t p -> n p t"))
 
         def x_back(pair, i):
             ps_x = bank(i, [P, 2, 4, P], BF16, "ps_x%d" % pair)
@@ -150,30 +150,37 @@ def tile_dcblock_w_kernel(
             for b in range(2):
                 nc.scalar.copy(out=x_nat[:, 2 * pair + b, :, :], in_=ps_x[:, b, :, :])
 
-        ps_t = [x_turn(0, 4), x_turn(1, 3)]
         hot = keep.tile([P, ROWS], F32)
         m2 = keep.tile([P, 1], F32)
         wrow_i = keep.tile([P, 1], I32)
         wrow = keep.tile([P, 1], F32)
         dw = keep.tile([P, P], F32)
         mask = keep.tile([P, P], F32)
-        nc.vector.tensor_copy(out=ident_f[:], in_=ident_b[:])
-        ones = keep.tile([P, P], F32)
-        nc.vector.memset(ones[:], 1.0)
-        other = keep.tile([P, 136], F32)
-        nc.vector.memset(other[:], 1.0)
-        nc.vector.tensor_scalar(out=other[:, 0:P], in0=ident_f[:], scalar1=-1.0, scalar2=1.0, op0=ALU.mult, op1=ALU.add)
+        n_out = keep.tile([P, 1], F32)
         lop = slice(0, KD)
+        ones = keep.tile([P, P], F32)
+        other = keep.tile([P, 136], F32)
         nc.vector.tensor_scalar(out=sel[:], in0=sel[:], scalar1=0.0, scalar2=None, op0=ALU.is_equal)
+        nc.vector.tensor_copy(out=ident_f[:], in_=ident_b[:])
         nc.vector.tensor_reduce(out=hot[:], in_=sel[:], axis=AX.X, op=ALU.add)
+        nc.vector.memset(ones[:], 1.0)
         nc.vector.memset(hot[64:64 + ROWS, :], 0.0)
+        nc.vector.memset(other[:], 1.0)
         nc.vector.tensor_scalar(out=m2[:], in0=hot[:, 1:2], scalar1=-2.0, scalar2=None, op0=ALU.mult)
         nc.vector.tensor_copy(out=dr[lop, OUTC:OUTC + 1], in_=hot[lop, 0:1])
-        nc.vector.tensor_single_scalar(out=wrow_i[:], in_=pidx[:], scalar=15, op=ALU.bitwise_and)
-        nc.vector.tensor_copy(out=wrow[:], in_=wrow_i[:])
-        nc.vector.tensor_tensor(out=dlin[:], in0=dlin[:], in1=dlin[:], op=ALU.mult)
-        nc.vector.tensor_scalar(out=dw[:], in0=wcol[:].rearrange("p h w -> p (h w)"), scalar1=wrow[:, 0:1],
-                                scalar2=None, op0=ALU.subtract)
+        nc.vector.tensor_tensor(out=sq[lop, :], in0=p4[lop, :], in1=p4[lop, :], op=ALU.mult)
+        nc.vector.tensor_scalar(out=lt[lop, :], in0=p4[lop, :], scalar1=m2[lop, 0:1], scalar2=hot[lop, 2:3],
+                                op0=ALU.mult, op1=ALU.add)
+        nc.vector.tensor_scalar(out=rt1[lop, :], in0=p4[lop, :], scalar1=hot[lop, 1:2], scalar2=hot[lop, 0:1],
+                                op0=ALU.mult, op1=ALU.add)
+        nc.vector.scalar_tensor_tensor(out=dl[lop, :], in0=sq[lop, :], scalar=hot[lop, 0:1], in1=lt[lop, :],
+                                       op0=ALU.mult, op1=ALU.add)
+        nc.vector.scalar_tensor_tensor(out=dr[lop, 0:P], in0=sq[lop, :], scalar=hot[lop, 2:3], in1=rt1[lop, :],
+                                       op0=ALU.mult, op1=ALU.add)
+        ps_d = bank(5, [P, 136], F32, "ps_d")
+        nc.tensor.matmul(ps_d[:, 0:OUTC + 1], lhsT=dl[:], rhs=dr[:, 0:OUTC + 1], start=True, stop=True)
+        ps_t = [x_turn(0, 4), x_turn(1, 3)]
+
         rs = keep.tile([P, G * T], F32)
         bn = keep.tile([P, 4, G * T], F32)
         mg = keep.tile([P, G * T], F32)
@@ -182,16 +189,20 @@ def tile_dcblock_w_kernel(
         bi = keep.tile([P, G * T], F32)
         nc.scalar.activation(out=rs[:].rearrange("p (g t) -> p g t", t=T),
                              in_=ps_bn[:, :, 0:8:2].rearrange("p t r -> p r t"), func=ACT.Sqrt, bias=BN_EPS)
+        nc.scalar.activation(out=warm[:], in_=warm[:], func=ACT.Exp)
         nc.vector.tensor_copy(
             out=bn[:].rearrange("p v (g t) -> p (v g) t", t=T),
             in_=ps_bn[:, :, 0:32:2].rearrange("p t r -> p r t"),
         )
         nc.vector.reciprocal(out=rs[:], in_=rs[:])
         nc.vector.tensor_tensor(out=mg[:], in0=bn[:, 1, :], in1=bn[:, 2, :], op=ALU.mult)
+        nc.vector.tensor_single_scalar(out=wrow_i[:], in_=pidx[:], scalar=15, op=ALU.bitwise_and)
         nc.vector.tensor_tensor(out=sc[:], in0=rs[:], in1=bn[:, 1, :], op=ALU.mult)
         nc.vector.tensor_tensor(out=nt[:], in0=rs[:], in1=mg[:], op=ALU.mult)
-        nc.vector.tensor_scalar(out=dlin[:], in0=dlin[:], scalar1=2652.25, scalar2=None, op0=ALU.is_le)
+        nc.vector.tensor_copy(out=wrow[:], in_=wrow_i[:])
+        nc.vector.tensor_scalar(out=other[:, 0:P], in0=ident_f[:], scalar1=-1.0, scalar2=1.0, op0=ALU.mult, op1=ALU.add)
         nc.vector.tensor_tensor(out=bi[:], in0=bn[:, 3, :], in1=nt[:], op=ALU.subtract)
+        nc.vector.tensor_tensor(out=dlin[:], in0=dlin[:], in1=dlin[:], op=ALU.mult)
 
         def bn_apply(g):
             for t in range(T):
@@ -214,49 +225,47 @@ def tile_dcblock_w_kernel(
                 in_=xg[:, g, :, :].rearrange("p n t -> p (n t)"),
             )
 
-        for g in (1, 2, 3):
-            bn_apply_scalar(g)
-        nc.scalar.activation(out=warm[:], in_=warm[:], func=ACT.Exp)
-        bn_apply(0)
-        nc.vector.tensor_tensor(out=sq[lop, :], in0=p4[lop, :], in1=p4[lop, :], op=ALU.mult)
-        regroup(0)
-        nc.vector.tensor_scalar(out=lt[lop, :], in0=p4[lop, :], scalar1=m2[lop, 0:1], scalar2=hot[lop, 2:3],
-                                op0=ALU.mult, op1=ALU.add)
-        quantise_x(0)
-        nc.vector.tensor_scalar(out=rt1[lop, :], in0=p4[lop, :], scalar1=hot[lop, 1:2], scalar2=hot[lop, 0:1],
-                                op0=ALU.mult, op1=ALU.add)
-        nc.vector.scalar_tensor_tensor(out=dl[lop, :], in0=sq[lop, :], scalar=hot[lop, 0:1], in1=lt[lop, :],
-                                       op0=ALU.mult, op1=ALU.add)
-        regroup(1)
-        x_turn_out(0, ps_t[0])
-        nc.vector.tensor_copy(out=dr[SIGR:SIGR + 1, SIGC:SIGC + 1], in_=p4[SIGR:SIGR + 1, 0:1])
-        nc.vector.scalar_tensor_tensor(out=dr[lop, 0:P], in0=sq[lop, :], scalar=hot[lop, 2:3], in1=rt1[lop, :],
-                                       op0=ALU.mult, op1=ALU.add)
-        quantise_x(1)
-        nc.vector.tensor_tensor(out=dw[:], in0=dw[:], in1=dw[:], op=ALU.mult)
-        regroup(2)
-        x_turn_out(1, ps_t[1])
-        nc.vector.scalar_tensor_tensor(out=mask[:], in0=dw[:], scalar=9.5, in1=dlin[:], op0=ALU.is_le, op1=ALU.mult)
-
-        ps_d = bank(5, [P, 136], F32, "ps_d")
         den = keep.tile([P, 1], F32)
         ex = keep.tile([P, 136], F32)
-
-        def distances():
-            nc.tensor.matmul(ps_d[:, 0:SIGC + 1], lhsT=dl[:], rhs=dr[:, 0:SIGC + 1], start=True, stop=True)
-
-        def affinity():
-            nc.vector.tensor_scalar(out=den[:], in0=ps_d[:, SIGC:SIGC + 1], scalar1=0.0, scalar2=None, op0=ALU.max)
-            quantise_x(2)
-            nc.vector.tensor_tensor(out=den[:], in0=den[:], in1=den[:], op=ALU.mult)
-            nc.vector.tensor_scalar(out=den[:], in0=den[:], scalar1=-2.0, scalar2=-1e-8, op0=ALU.mult, op1=ALU.add)
-            regroup(3)
-            nc.vector.reciprocal(out=den[:], in_=den[:])
-            nc.vector.scalar_tensor_tensor(out=ex[:, 0:129], in0=ps_d[:, 0:129], scalar=0.0, in1=other[:, 0:129],
-                                           op0=ALU.max, op1=ALU.mult)
-            nc.scalar.activation(out=ex[:, 0:129], in_=ex[:, 0:129], func=ACT.Exp, scale=den[:, 0:1])
-            nc.scalar.activation(out=ex[:, 0:129], in_=ex[:, 0:129], func=ACT.Exp, bias=-1.0)
-            quantise_x(3)
+        aff = keep.tile([P, P], F32)
+        own = keep.tile([P, 1], F32)
+        aff_s = keep.tile([P, P], F32)
+        rsum = keep.tile([P, P], F32)
+        bn_apply_scalar(1)
+        bn_apply_scalar(2)
+        bn_apply(0)
+        nc.vector.tensor_scalar(out=dw[:], in0=wcol[:].rearrange("p h w -> p (h w)"), scalar1=wrow[:, 0:1],
+                                scalar2=None, op0=ALU.subtract)
+        regroup(0)
+        nc.vector.scalar_tensor_tensor(out=ex[:, 0:129], in0=ps_d[:, 0:129], scalar=0.0, in1=other[:, 0:129],
+                                       op0=ALU.max, op1=ALU.mult)
+        quantise_x(0)
+        nc.vector.tensor_copy(out=dr[SIGR:SIGR + 1, SIGC:SIGC + 1], in_=p4[SIGR:SIGR + 1, 0:1])
+        nc.tensor.matmul(ps_d[:, SIGC:SIGC + 2], lhsT=ones[:], rhs=dr[:, SIGC:SIGC + 2], start=True, stop=True)
+        nc.vector.tensor_scalar(out=dlin[:], in0=dlin[:], scalar1=2652.25, scalar2=None, op0=ALU.is_le)
+        regroup(1)
+        nc.vector.tensor_tensor(out=dw[:], in0=dw[:], in1=dw[:], op=ALU.mult)
+        nc.vector.tensor_scalar(out=den[:], in0=ps_d[:, SIGC:SIGC + 1], scalar1=0.0, scalar2=None, op0=ALU.max)
+        quantise_x(1)
+        nc.vector.tensor_tensor(out=den[:], in0=den[:], in1=den[:], op=ALU.mult)
+        nc.vector.scalar_tensor_tensor(out=mask[:], in0=dw[:], scalar=9.5, in1=dlin[:], op0=ALU.is_le, op1=ALU.mult)
+        nc.vector.tensor_scalar(out=den[:], in0=den[:], scalar1=-2.0, scalar2=-1e-8, op0=ALU.mult, op1=ALU.add)
+        regroup(2)
+        nc.vector.reciprocal(out=den[:], in_=den[:])
+        nc.scalar.activation(out=ex[:, 0:129], in_=ex[:, 0:129], func=ACT.Exp, scale=den[:, 0:1])
+        nc.scalar.activation(out=ex[:, 0:129], in_=ex[:, 0:129], func=ACT.Exp, bias=-1.0)
+        for pair in range(2):
+            x_turn_out(pair, ps_t[pair])
+        bn_apply_scalar(3)
+        nc.vector.tensor_reduce(out=n_out[:], in_=mask[:], axis=AX.X, op=ALU.add)
+        quantise_x(2)
+        nc.vector.tensor_scalar(out=n_out[:], in0=n_out[:], scalar1=-1.0, scalar2=49.0, op0=ALU.mult, op1=ALU.add)
+        nc.vector.tensor_tensor(out=aff[:], in0=ex[:, 0:P], in1=mask[:], op=ALU.mult)
+        nc.vector.tensor_tensor(out=own[:], in0=ex[:, 128:129], in1=n_out[:], op=ALU.mult)
+        nc.vector.scalar_tensor_tensor(out=aff_s[:], in0=ident_f[:], scalar=own[:, 0:1], in1=aff[:],
+                                       op0=ALU.mult, op1=ALU.add)
+        regroup(3)
+        quantise_x(3)
 
         mt = keep.tile([P, G, T, P], F32)
         m_bank = (6, 7, 0, 1)
@@ -296,29 +305,14 @@ def tile_dcblock_w_kernel(
                 in_=ag[:, c, :, :].rearrange("p n t -> p (n t)"),
             )
 
-        messages((0,), range(G))
-        distances()
-        affinity()
-        ps_x = [x_back(0, 2), x_back(1, 4)]
-        messages((1, 2), range(G))
-        for pair in range(2):
-            x_back_out(pair, ps_x[pair])
-
-        n_out = keep.tile([P, 1], F32)
-        aff = keep.tile([P, P], F32)
-        own = keep.tile([P, 1], F32)
-        aff_s = keep.tile([P, P], F32)
-        rsum = keep.tile([P, P], F32)
-        nc.vector.tensor_reduce(out=n_out[:], in_=mask[:], axis=AX.X, op=ALU.add)
-        nc.vector.tensor_scalar(out=n_out[:], in0=n_out[:], scalar1=-1.0, scalar2=49.0, op0=ALU.mult, op1=ALU.add)
-        nc.vector.tensor_tensor(out=aff[:], in0=ex[:, 0:P], in1=mask[:], op=ALU.mult)
-        nc.vector.tensor_tensor(out=own[:], in0=ex[:, 128:129], in1=n_out[:], op=ALU.mult)
-        nc.vector.scalar_tensor_tensor(out=aff_s[:], in0=ident_f[:], scalar=own[:, 0:1], in1=aff[:],
-                                       op0=ALU.mult, op1=ALU.add)
+        messages((0, 1), range(G))
         ps_s = bank(5, [P, P], F32, "ps_s")
         nc.tensor.matmul(ps_s[:], lhsT=ones[:], rhs=aff_s[:], start=True, stop=True)
-        messages((3,), range(G))
         nc.vector.reciprocal(out=rsum[:], in_=ps_s[:])
+        ps_x = [x_back(0, 2), x_back(1, 4)]
+        for pair in range(2):
+            x_back_out(pair, ps_x[pair])
+        messages((2, 3), range(G))
         for c in range(G):
             messages_out(c)
         ps_a0 = aggregate(0)
@@ -356,10 +350,9 @@ def tile_dcblock_w_kernel(
             return [bank(i, [P, P], F32, "ps_r%d%d" % (c, j)) for j, i in enumerate(banks)]
 
         ps_r = [tiles(0, (6, 7, 0, 1)), tiles(1, (2, 3, 4, 5))]
-        for gs in ((0, 1, 2), (3,)):
-            for c in range(2):
-                for j in range(4):
-                    refine(ps_r[c][j], c, j, gs)
+        for c, gs in ((0, (0, 1, 2)), (1, (0, 1)), (0, (3,)), (1, (2, 3))):
+            for j in range(4):
+                refine(ps_r[c][j], c, j, gs)
         for c in range(2):
             for j in range(4):
                 add_x(ps_r[c][j], c, j)

from contextlib import ExitStack

import concourse.mybir as mybir
from concourse.masks import make_identity

F32 = mybir.dt.float32
BF16 = mybir.dt.bfloat16
I32 = mybir.dt.int32
U32 = mybir.dt.uint32
U8 = mybir.dt.uint8
FP8X4 = mybir.dt.float8_e4m3fn_x4
ALU = mybir.AluOpType
ACT = mybir.ActivationFunctionType
AX = mybir.AxisListType

P = 128
C = 2048
G = 4
T = 4
CP = 19
NCH = 512
HALF = 1024
BN_EPS = 1e-5

ROWS = 4
KD = ROWS * (CP + 1)
SIGR = 96
OUTC = P
SIGC = P + 2

FLOPS = 2 * 2 * C * C * P + 2 * 49 * C * P


def tile_dcblock_w_kernel(
    tc, x, coarse_probs, sigma, w_feat_words, w_feat_scales, w_fuse_words, w_fuse_scales,
    bn_gamma, bn_beta, bn_mean, bn_var, out,
):
    nc = tc.nc
    with ExitStack() as ctx:
        ctx.enter_context(tc.manual_schedule())
        keep = ctx.enter_context(tc.tile_pool(name="keep", bufs=1))
        psum = ctx.enter_context(tc.psum_pool(name="psum", bufs=1))

        def bank(i, shape, dtype, name):
            return psum.tile(shape, dtype, tag="b%d" % i, name=name)

        wf_words = keep.tile([P, G, C], U32, align_bytes=64)
        wu_words = keep.tile([P, G, C], U32, align_bytes=64)
        wf_planes = keep.tile([P, C], U8, align_bytes=64)
        wu_planes = keep.tile([P, C], U8, align_bytes=64)
        x_sb = keep.tile([P, G, T, P], BF16, align_bytes=64)
        xn = keep.tile([P, G, T, P], BF16, align_bytes=64)
        xg = keep.tile([P, G, P, T], BF16, align_bytes=64)
        xq_words = keep.tile([P, G, P], U32, align_bytes=64)
        xq_planes = keep.tile([P, G, P], U8, align_bytes=64)
        ag = keep.tile([P, G, P, T], BF16, align_bytes=64)
        aq_words = keep.tile([P, G, P], U32, align_bytes=64)
        aq_planes = keep.tile([P, G, P], U8, align_bytes=64)
        small = keep.tile([P, 512], BF16, align_bytes=64)
        p4 = keep.tile([P, P], BF16, align_bytes=64)
        sq = keep.tile([P, P], F32)
        dl = keep.tile([P, P], F32, align_bytes=64)
        dr = keep.tile([P, 136], F32, align_bytes=64)
        lt = keep.tile([P, P], F32)
        rt1 = keep.tile([P, P], F32)
        ident_b = keep.tile([P, P], BF16, align_bytes=64)
        ident_f = keep.tile([P, P], F32, align_bytes=64)
        x_t = keep.tile([P, G, P, T], BF16)
        x_nat = keep.tile([P, G, 4, P], BF16)

        def load_planes(planes, scales):
            for q in range(4):
                nc.sync.dma_start(
                    out=planes[32 * q:32 * q + 16, :].bitcast(I32),
                    in_=scales[:, 4 * q:4 * q + 4, :].bitcast(I32),
                )

        def load_words(words, dram, g0, gn, c0, cn):
            nc.sync.dma_start(
                out=words[:, g0:g0 + gn, c0:c0 + cn].bitcast(I32),
                in_=dram.rearrange("g p n t -> p g (n t)")[:, g0:g0 + gn, T * c0:T * (c0 + cn)].bitcast(I32),
            )

        warm = keep.tile([P, 1], F32)
        nc.vector.memset(warm[:], 1.0)
        nc.vector.memset(wf_planes[:].bitcast(I32), 0)
        nc.vector.memset(small[32:64, :].bitcast(I32), 0)
        nc.vector.memset(small[64:P, :].bitcast(I32), 0)
        nc.vector.memset(dr[:], 0.0)
        nc.vector.memset(wu_planes[:].bitcast(I32), 0)
        nc.vector.memset(dl[:], 1.0)
        for v, vec in enumerate((bn_var, bn_gamma, bn_mean, bn_beta)):
            nc.sync.dma_start(out=small[8 * v:8 * v + 8, :],
                              in_=vec.rearrange("(g k) -> g k", g=G).unsqueeze(1).to_broadcast([G, 2, 512]))
        nc.sync.dma_start(
            out=x_sb[:].rearrange("p g t n -> p g (t n)"),
            in_=x.rearrange("b (g p t) h w -> p (b g) (t h w)", p=P, t=T),
        )
        for r0, c0, c1 in ((0, 0, 16), (64, 15, CP)):
            nc.scalar.dma_start(
                out=p4[r0:r0 + ROWS * (c1 - c0), :],
                in_=coarse_probs.rearrange("b c h w -> (b c) (h w)")[c0:c1].unsqueeze(1).to_broadcast([c1 - c0, ROWS, P]),
            )
        nc.scalar.activation(out=warm[:], in_=warm[:], func=ACT.Sqrt)
        load_words(wf_words, w_feat_words, 0, 1, 0, C)
        load_planes(wf_planes, w_feat_scales)
        load_words(wf_words, w_feat_words, 1, 1, 0, C)
        nc.scalar.dma_start(out=p4[SIGR:SIGR + 1, 0:1], in_=sigma.unsqueeze(0))
        load_words(wf_words, w_feat_words, 2, 1, 0, C)
        load_words(wf_words, w_feat_words, 3, 1, 0, C)
        load_planes(wu_planes, w_fuse_scales)
        for piece in ((0, 4, 0, HALF), (0, 2, HALF, HALF), (2, 2, HALF, NCH), (2, 2, HALF + NCH, NCH)):
            load_words(wu_words, w_fuse_words, *piece)

        make_identity(nc, ident_b[:])
        sel = keep.tile([P, ROWS, CP + 1], F32)
        nc.gpsimd.iota(sel[:], pattern=[[1, ROWS], [ROWS, CP + 1]], base=0, channel_multiplier=-1,
                       allow_small_or_imprecise_dtypes=True)
        pidx = keep.tile([P, 1], I32)
        nc.gpsimd.iota(pidx[:], pattern=[[0, 1]], base=0, channel_multiplier=1)
        wcol = keep.tile([P, 8, 16], F32)
        nc.gpsimd.iota(wcol[:], pattern=[[0, 8], [1, 16]], base=0, channel_multiplier=0,
                       allow_small_or_imprecise_dtypes=True)
        dlin = keep.tile([P, P], F32)
        nc.gpsimd.iota(dlin[:], pattern=[[1, P]], base=0, channel_multiplier=-1,
                       allow_small_or_imprecise_dtypes=True)

        ps_bn = bank(6, [P, T, P], BF16, "ps_bn")
        for t in range(T):
            nc.tensor.transpose(ps_bn[:, t, :], small[:, t:512:T], ident_b[:])
        def x_turn(pair, i):
            ps_t = bank(i, [P, 2, T, P], BF16, "ps_t%d" % pair)
            for b in range(2):
                for t in range(T):
                    nc.tensor.transpose(ps_t[:, b, t, :], x_sb[:, 2 * pair + b, t, :], ident_b[:])
            return ps_t

        def x_turn_out(pair, ps_t):
            for b in range(2):
                nc.scalar.copy(out=x_t[:, 2 * pair + b, :, :], in_=ps_t[:, b, :, :].rearrange("n t p -> n p t"))

        def x_back(pair, i):
            ps_x = bank(i, [P, 2, 4, P], BF16, "ps_x%d" % pair)
            for b in range(2):
                for j in range(4):
                    nc.tensor.transpose(ps_x[:, b, j, :], x_t[:, 2 * pair + b, 32 * j:32 * (j + 1), :].rearrange("n p t -> n (p t)"), ident_b[:])
            return ps_x

        def x_back_out(pair, ps_x):
            for b in range(2):
                nc.scalar.copy(out=x_nat[:, 2 * pair + b, :, :], in_=ps_x[:, b, :, :])

        hot = keep.tile([P, ROWS], F32)
        m2 = keep.tile([P, 1], F32)
        wrow_i = keep.tile([P, 1], I32)
        wrow = keep.tile([P, 1], F32)
        dw = keep.tile([P, P], F32)
        mask = keep.tile([P, P], F32)
        n_out = keep.tile([P, 1], F32)
        lop = slice(0, KD)
        ones = keep.tile([P, P], F32)
        other = keep.tile([P, 136], F32)
        nc.vector.tensor_scalar(out=sel[:], in0=sel[:], scalar1=0.0, scalar2=None, op0=ALU.is_equal)
        nc.vector.tensor_copy(out=ident_f[:], in_=ident_b[:])
        nc.vector.tensor_reduce(out=hot[:], in_=sel[:], axis=AX.X, op=ALU.add)
        nc.vector.memset(ones[:], 1.0)
        nc.vector.memset(hot[64:64 + ROWS, :], 0.0)
        nc.vector.memset(other[:], 1.0)
        nc.vector.tensor_scalar(out=m2[:], in0=hot[:, 1:2], scalar1=-2.0, scalar2=None, op0=ALU.mult)
        nc.vector.tensor_copy(out=dr[lop, OUTC:OUTC + 1], in_=hot[lop, 0:1])
        nc.vector.tensor_tensor(out=sq[lop, :], in0=p4[lop, :], in1=p4[lop, :], op=ALU.mult)
        nc.vector.tensor_scalar(out=lt[lop, :], in0=p4[lop, :], scalar1=m2[lop, 0:1], scalar2=hot[lop, 2:3],
                                op0=ALU.mult, op1=ALU.add)
        nc.vector.tensor_scalar(out=rt1[lop, :], in0=p4[lop, :], scalar1=hot[lop, 1:2], scalar2=hot[lop, 0:1],
                                op0=ALU.mult, op1=ALU.add)
        nc.vector.scalar_tensor_tensor(out=dl[lop, :], in0=sq[lop, :], scalar=hot[lop, 0:1], in1=lt[lop, :],
                                       op0=ALU.mult, op1=ALU.add)
        nc.vector.scalar_tensor_tensor(out=dr[lop, 0:P], in0=sq[lop, :], scalar=hot[lop, 2:3], in1=rt1[lop, :],
                                       op0=ALU.mult, op1=ALU.add)
        ps_d = bank(5, [P, 136], F32, "ps_d")
        nc.tensor.matmul(ps_d[:, 0:OUTC + 1], lhsT=dl[:], rhs=dr[:, 0:OUTC + 1], start=True, stop=True)
        ps_t = [x_turn(0, 4), x_turn(1, 3)]

        rs = keep.tile([P, G * T], F32)
        bn = keep.tile([P, 4, G * T], F32)
        mg = keep.tile([P, G * T], F32)
        nt = keep.tile([P, G * T], F32)
        sc = keep.tile([P, G * T], F32)
        bi = keep.tile([P, G * T], F32)
        nc.scalar.activation(out=rs[:].rearrange("p (g t) -> p g t", t=T),
                             in_=ps_bn[:, :, 0:8:2].rearrange("p t r -> p r t"), func=ACT.Sqrt, bias=BN_EPS)
        nc.scalar.activation(out=warm[:], in_=warm[:], func=ACT.Exp)
        nc.vector.tensor_copy(
            out=bn[:].rearrange("p v (g t) -> p (v g) t", t=T),
            in_=ps_bn[:, :, 0:32:2].rearrange("p t r -> p r t"),
        )
        nc.vector.reciprocal(out=rs[:], in_=rs[:])
        nc.vector.tensor_tensor(out=mg[:], in0=bn[:, 1, :], in1=bn[:, 2, :], op=ALU.mult)
        nc.vector.tensor_single_scalar(out=wrow_i[:], in_=pidx[:], scalar=15, op=ALU.bitwise_and)
        nc.vector.tensor_tensor(out=sc[:], in0=rs[:], in1=bn[:, 1, :], op=ALU.mult)
        nc.vector.tensor_tensor(out=nt[:], in0=rs[:], in1=mg[:], op=ALU.mult)
        nc.vector.tensor_copy(out=wrow[:], in_=wrow_i[:])
        nc.vector.tensor_scalar(out=other[:, 0:P], in0=ident_f[:], scalar1=-1.0, scalar2=1.0, op0=ALU.mult, op1=ALU.add)
        nc.vector.tensor_tensor(out=bi[:], in0=bn[:, 3, :], in1=nt[:], op=ALU.subtract)
        nc.vector.tensor_tensor(out=dlin[:], in0=dlin[:], in1=dlin[:], op=ALU.mult)

        def bn_apply(g):
            for t in range(T):
                k = g * T + t
                nc.vector.tensor_scalar(out=xn[:, g, t, :], in0=x_sb[:, g, t, :], scalar1=sc[:, k:k + 1],
                                        scalar2=bi[:, k:k + 1], op0=ALU.mult, op1=ALU.add)

        def bn_apply_scalar(g):
            for t in range(T):
                k = g * T + t
                nc.scalar.activation(out=xn[:, g, t, :], in_=x_sb[:, g, t, :], func=ACT.Identity,
                                     scale=sc[:, k:k + 1], bias=bi[:, k:k + 1])

        def regroup(g):
            nc.vector.tensor_copy(out=xg[:, g, :, :], in_=xn[:, g, :, :].rearrange("p t n -> p n t"))

        def quantise_x(g):
            nc.vector.quantize_mx(
                out=xq_words[:, g, :].bitcast(FP8X4), scales=xq_planes[:, g, :],
                in_=xg[:, g, :, :].rearrange("p n t -> p (n t)"),
            )

        den = keep.tile([P, 1], F32)
        ex = keep.tile([P, 136], F32)
        aff = keep.tile([P, P], F32)
        own = keep.tile([P, 1], F32)
        aff_s = keep.tile([P, P], F32)
        rsum = keep.tile([P, P], F32)
        bn_apply_scalar(1)
        bn_apply_scalar(2)
        bn_apply(0)
        nc.vector.tensor_scalar(out=dw[:], in0=wcol[:].rearrange("p h w -> p (h w)"), scalar1=wrow[:, 0:1],
                                scalar2=None, op0=ALU.subtract)
        regroup(0)
        nc.vector.scalar_tensor_tensor(out=ex[:, 0:129], in0=ps_d[:, 0:129], scalar=0.0, in1=other[:, 0:129],
                                       op0=ALU.max, op1=ALU.mult)
        quantise_x(0)
        nc.vector.tensor_copy(out=dr[SIGR:SIGR + 1, SIGC:SIGC + 1], in_=p4[SIGR:SIGR + 1, 0:1])
        nc.tensor.matmul(ps_d[:, SIGC:SIGC + 2], lhsT=ones[:], rhs=dr[:, SIGC:SIGC + 2], start=True, stop=True)
        nc.vector.tensor_scalar(out=dlin[:], in0=dlin[:], scalar1=2652.25, scalar2=None, op0=ALU.is_le)
        regroup(1)
        nc.vector.tensor_tensor(out=dw[:], in0=dw[:], in1=dw[:], op=ALU.mult)
        nc.vector.tensor_scalar(out=den[:], in0=ps_d[:, SIGC:SIGC + 1], scalar1=0.0, scalar2=None, op0=ALU.max)
        quantise_x(1)
        nc.vector.tensor_tensor(out=den[:], in0=den[:], in1=den[:], op=ALU.mult)
        nc.vector.scalar_tensor_tensor(out=mask[:], in0=dw[:], scalar=9.5, in1=dlin[:], op0=ALU.is_le, op1=ALU.mult)
        nc.vector.tensor_scalar(out=den[:], in0=den[:], scalar1=-2.0, scalar2=-1e-8, op0=ALU.mult, op1=ALU.add)
        regroup(2)
        nc.vector.reciprocal(out=den[:], in_=den[:])
        nc.scalar.activation(out=ex[:, 0:129], in_=ex[:, 0:129], func=ACT.Exp, scale=den[:, 0:1])
        nc.scalar.activation(out=ex[:, 0:129], in_=ex[:, 0:129], func=ACT.Exp, bias=-1.0)
        for pair in range(2):
            x_turn_out(pair, ps_t[pair])
        bn_apply_scalar(3)
        nc.vector.tensor_reduce(out=n_out[:], in_=mask[:], axis=AX.X, op=ALU.add)
        quantise_x(2)
        nc.vector.tensor_scalar(out=n_out[:], in0=n_out[:], scalar1=-1.0, scalar2=49.0, op0=ALU.mult, op1=ALU.add)
        nc.vector.tensor_tensor(out=aff[:], in0=ex[:, 0:P], in1=mask[:], op=ALU.mult)
        nc.vector.tensor_tensor(out=own[:], in0=ex[:, 128:129], in1=n_out[:], op=ALU.mult)
        nc.vector.scalar_tensor_tensor(out=aff_s[:], in0=ident_f[:], scalar=own[:, 0:1], in1=aff[:],
                                       op0=ALU.mult, op1=ALU.add)
        regroup(3)
        quantise_x(3)

        mt = keep.tile([P, G, T, P], F32)
        m_bank = (6, 7, 0, 1)
        ps_m = [bank(m_bank[c], [P, NCH], F32, "ps_m%d" % c) for c in range(G)]

        def messages(gs, cs):
            for g in gs:
                for c in cs:
                    cols = slice(c * NCH, (c + 1) * NCH)
                    nc.tensor.matmul_mx(
                        out=ps_m[c][:], lhsT=xq_words[:, g, :].bitcast(FP8X4), lhsT_scale=xq_planes[:, g, :],
                        rhs=wf_words[:, g, cols].bitcast(FP8X4), rhs_scale=wf_planes[4 * g:P, cols],
                        start=(g == 0), stop=(g == G - 1),
                    )

        def messages_out(c):
            src = ps_m[c][:].rearrange("q (p t) -> q t p", t=T)
            if c % 2:
                nc.vector.tensor_copy(out=mt[:, c, :, :], in_=src)
            else:
                for t in (0, 2):
                    nc.scalar.copy(out=mt[:, c, t:t + 2, :], in_=src[:, t:t + 2, :])

        def aggregate(c):
            ps_a = bank(2 + c, [P, T, P], F32, "ps_a%d" % c)
            for t in range(T):
                nc.tensor.matmul(ps_a[:, t, :], lhsT=mt[:, c, t, :], rhs=aff[:], start=True, stop=True)
            return ps_a

        def divide(c, ps_a):
            nc.vector.tensor_tensor(out=ag[:, c, :, :], in0=ps_a[:].rearrange("p t n -> p n t"),
                                    in1=rsum[:].unsqueeze(2).to_broadcast([P, P, T]), op=ALU.mult)

        def quantise_agg(c):
            nc.vector.quantize_mx(
                out=aq_words[:, c, :].bitcast(FP8X4), scales=aq_planes[:, c, :],
                in_=ag[:, c, :, :].rearrange("p n t -> p (n t)"),
            )

        messages((0, 1), range(G))
        ps_s = bank(5, [P, P], F32, "ps_s")
        nc.tensor.matmul(ps_s[:], lhsT=ones[:], rhs=aff_s[:], start=True, stop=True)
        nc.vector.reciprocal(out=rsum[:], in_=ps_s[:])
        ps_x = [x_back(0, 2), x_back(1, 4)]
        for pair in range(2):
            x_back_out(pair, ps_x[pair])
        messages((2, 3), range(G))
        for c in range(G):
            messages_out(c)
        ps_a0 = aggregate(0)
        ps_a1 = aggregate(1)
        divide(0, ps_a0)
        ps_a2 = aggregate(2)
        quantise_agg(0)
        divide(1, ps_a1)
        ps_a3 = aggregate(3)
        quantise_agg(1)
        divide(2, ps_a2)
        quantise_agg(2)
        divide(3, ps_a3)
        quantise_agg(3)

        o_sb = keep.tile([P, G, 4, P], F32)
        out_d = out.rearrange("b (c j p) h w -> p (b c) j (h w)", p=P, j=4)

        def refine(tile, c, j, gs):
            cols = slice(c * NCH + j * P, c * NCH + (j + 1) * P)
            for g in gs:
                nc.tensor.matmul_mx(
                    out=tile[:], lhsT=wu_words[:, g, cols].bitcast(FP8X4), lhsT_scale=wu_planes[4 * g:P, cols],
                    rhs=aq_words[:, g, :].bitcast(FP8X4), rhs_scale=aq_planes[:, g, :],
                    start=(g == 0), stop=(g == G - 1),
                )

        def add_x(tile, c, j):
            nc.vector.tensor_tensor(out=o_sb[:, c, j, :], in0=tile[:], in1=x_nat[:, c, j, :], op=ALU.add)

        def store(c, j0, j1):
            nc.sync.dma_start(out=out_d[:, c, j0:j1, :], in_=o_sb[:, c, j0:j1, :])

        def tiles(c, banks):
            return [bank(i, [P, P], F32, "ps_r%d%d" % (c, j)) for j, i in enumerate(banks)]

        ps_r = [tiles(0, (6, 7, 0, 1)), tiles(1, (2, 3, 4, 5))]
        for c, gs in ((0, (0, 1, 2)), (1, (0, 1)), (0, (3,)), (1, (2, 3))):
            for j in range(4):
                refine(ps_r[c][j], c, j, gs)
        for c in range(2):
            for j in range(4):
                add_x(ps_r[c][j], c, j)
            store(c, 0, 4)
        ps_r = {2: tiles(2, (6, 7, 0, 1)), 3: tiles(3, (2, 3, 4, 5))}
        for c in (2, 3):
            for gs in ((0, 1), (2, 3)):
                for j in range(4):
                    refine(ps_r[c][j], c, j, gs)
            for j in range(4):
                add_x(ps_r[c][j], c, j)
                if c == 3 and j == 1:
                    store(3, 0, 2)
            store(c, 2 * (c - 2), 4)
